import numpy as np
import ml_dtypes


def mxq(x, axis, fmt="e4m3"):
    dtype, down = {"e4m3": (ml_dtypes.float8_e4m3fn, 7), "e5m2": (ml_dtypes.float8_e5m2, 14)}[fmt]
    v = np.moveaxis(np.asarray(x, np.float32).astype(ml_dtypes.bfloat16).astype(np.float64), axis, -1)
    blocks = v.reshape(v.shape[:-1] + (-1, 32))
    amax = np.abs(blocks).max(-1, keepdims=True)
    byte = np.maximum(np.where(amax > 0, np.frexp(amax)[1] - 1 + 127, 0) - down, 1)
    scale = np.exp2(byte - 127.0)
    codes = (blocks / scale).astype(np.float32).astype(dtype).astype(np.float64)
    return np.moveaxis((codes * scale).reshape(v.shape), -1, axis)


WIDE = False


def mx_kscale(k):
    if not WIDE:
        return np.ones(k)
    levels = np.array([10, -10, 5, -5, 0])
    if k % 512:
        return np.exp2(np.random.permutation(np.resize(levels, k // 32))).repeat(32)
    a = np.empty((k // 512, 16))
    for p in range(k // 512):
        a[p, :8] = np.random.permutation(np.resize(levels, 8))
        for g in range(8):
            far = levels[np.abs(levels - a[p, g]) >= 10]
            a[p, g + 8] = far[np.random.randint(len(far))]
    return np.exp2(a.ravel()).repeat(32)


BF16 = ml_dtypes.bfloat16


def bf(x):
    return np.asarray(x, np.float32).astype(BF16)


def f64(x):
    return np.asarray(x).astype(np.float64)


B, S, D, E = 4, 512, 1024, 1024
THETA = 10000.0


def rope_tables():
    inv = 1.0 / THETA ** (np.arange(0, E, 2).astype(np.float64) / E)
    ang = np.outer(np.arange(S).astype(np.float64), inv)
    return np.cos(ang), np.sin(ang)


def rotate(u, cos, sin):
    ur, ui = u[..., 0::2], u[..., 1::2]
    return np.stack([ur * cos - ui * sin, ur * sin + ui * cos], axis=-1).reshape(B, S, E)


def draw0():
    s = mx_kscale(D)
    return {"x": bf(np.random.standard_normal((B, S, D)) * s),
            "wq": bf(np.random.standard_normal((E, D)) / np.sqrt(D) / s),
            "wk": bf(np.random.standard_normal((E, D)) / np.sqrt(D) / s)}


def core(x, wq, wk):
    xm = mxq(f64(x), 2, "e4m3")
    xq = xm @ mxq(f64(wq), 1, "e4m3").T
    xk = xm @ mxq(f64(wk), 1, "e4m3").T
    cos, sin = rope_tables()
    return rotate(xq, cos, sin), rotate(xk, cos, sin)


def e4m3fn_bytes(y):
    return np.clip(np.asarray(y, np.float64), -448.0, 448.0).astype(np.float32).astype(ml_dtypes.float8_e4m3fn).view(np.uint8)


def e4m3fn_values(b):
    return np.asarray(b, np.uint8).view(ml_dtypes.float8_e4m3fn).astype(np.float64)


def setup_inputs():
    d = draw0()
    x0 = np.asarray(d['x']).astype(np.float64)
    s = (np.max(np.abs(x0), axis=(0, 1), keepdims=True) / 448.0).astype(np.float32)
    out = {}
    for k, v in d.items():
        if k == 'x':
            out['x_bytes'] = e4m3fn_bytes(x0 / s.astype(np.float64))
            out['x_scale'] = s
        else:
            out[k] = v
    return out


def reference(x_bytes, x_scale, wq, wk):
    return core(e4m3fn_values(x_bytes) * x_scale.astype(np.float64), wq, wk)

@@ -1,0 +1,322 @@
+from contextlib import ExitStack
+import math
+
+import concourse.mybir as mybir
+from concourse.masks import make_identity
+
+B, S, D, E = 4, 512, 1024, 1024
+THETA = 10000.0
+FLOPS = 2 * B * S * D * 2 * E
+
+F32 = mybir.dt.float32
+BF16 = mybir.dt.bfloat16
+I32 = mybir.dt.int32
+U32 = mybir.dt.uint32
+U8 = mybir.dt.uint8
+FP8 = mybir.dt.float8_e4m3fn
+FP8X4 = mybir.dt.float8_e4m3fn_x4
+ALU = mybir.AluOpType
+ACT = mybir.ActivationFunctionType
+
+P = 128
+PAIRS = E // 2
+POS_TILES = S // P
+PASSES = D // 512
+TWO_PI = 2.0 * math.pi
+REDUCED = 288
+
+
+def tile_attention_pa_kernel(tc, x_bytes, x_scale, wq, wk, out_0, out_1):
+    nc = tc.nc
+    outs = (out_0, out_1)
+    weights = (wq, wk)
+
+    with ExitStack() as ctx:
+        const = ctx.enter_context(tc.tile_pool(name="const", bufs=1))
+        tabtmp = ctx.enter_context(tc.tile_pool(name="tabtmp", bufs=2))
+        xwp = ctx.enter_context(tc.tile_pool(name="xwp", bufs=3))
+        xgp = ctx.enter_context(tc.tile_pool(name="xgp", bufs=3))
+        xcp = ctx.enter_context(tc.tile_pool(name="xcp", bufs=1))
+        xg4p = ctx.enter_context(tc.tile_pool(name="xg4p", bufs=1))
+        wgp = ctx.enter_context(tc.tile_pool(name="wgp", bufs=2))
+        pqp = ctx.enter_context(tc.tile_pool(name="pqp", bufs=2))
+        op = ctx.enter_context(tc.tile_pool(name="op", bufs=2))
+        wrp = ctx.enter_context(tc.tile_pool(name="wrp", bufs=4))
+        tps = ctx.enter_context(tc.psum_pool(name="tps", bufs=2))
+        accp = ctx.enter_context(tc.psum_pool(name="accp", bufs=6))
+        ctx.enter_context(tc.manual_schedule(engines={mybir.EngineType.PE, mybir.EngineType.DVE}))
+
+        xs_bc = const.tile([P, D], F32, name="xs_bc")
+        nc.sync.dma_start(out=xs_bc[:], in_=x_scale.rearrange("a b k -> (a b k)").partition_broadcast(P))
+        xs_col = const.tile([P, PASSES, 4], F32, name="xs_col")
+        nc.sync.dma_start(out=xs_col[:], in_=x_scale.rearrange("a b k -> (a b k)").rearrange("(g p t) -> p g t", p=P, t=4))
+        xb_view = x_bytes.rearrange("b (a p) k -> a p b k", p=P)
+        xbytes = []
+        for a in range(POS_TILES):
+            xbytes_a = const.tile([P, B, D], U8, name="xbytes%d" % a)
+            xbytes.append(xbytes_a)
+        wraw = []
+
+        def load_x(a):
+            nc.sync.dma_start(out=xbytes[a][:], in_=xb_view[a])
+
+        def load_w(c):
+            src = weights[c // 2].rearrange("(r p e) k -> e p r k", p=P, e=2)
+            wraw_c = wrp.tile([P, 4, D], BF16, name="wraw")
+            wraw.append(wraw_c)
+            nc.sync.dma_start(out=wraw_c[:], in_=src[c % 2])
+
+        load_x(0)
+        load_w(0)
+        load_w(1)
+        load_x(1)
+        load_w(2)
+        load_w(3)
+        load_x(2)
+        load_x(3)
+
+        ident = const.tile([P, P], F32, name="ident")
+        make_identity(nc, ident[:])
+        tcol = const.tile([P, POS_TILES], F32, name="tcol")
+        nc.gpsimd.iota(tcol[:], pattern=[[P, POS_TILES]], base=0, channel_multiplier=1,
+                       allow_small_or_imprecise_dtypes=True)
+        turns = const.tile([P, POS_TILES], F32, name="turns")
+        nc.vector.tensor_scalar(out=turns[:], in0=tcol[:], scalar1=1.0 / TWO_PI, scalar2=None, op0=ALU.mult)
+        inv = const.tile([P, PAIRS], F32, name="inv")
+        nc.vector.memset(inv[:, 0:1], 1.0)
+        n = 1
+        while n < PAIRS:
+            nc.vector.tensor_scalar(out=inv[:, n:2 * n], in0=inv[:, 0:n], scalar1=THETA ** (-n / float(PAIRS)),
+                                    scalar2=None, op0=ALU.mult)
+            n *= 2
+
+        fracs = {}
+        tabs = {}
+
+        def table_turns(a):
+            tcolumn = turns[:, a:a + 1]
+            ni = tabtmp.tile([P, REDUCED], I32, name="ni")
+            nc.vector.tensor_scalar(out=ni[:], in0=inv[:, 0:REDUCED], scalar1=tcolumn, scalar2=None, op0=ALU.mult)
+            f = const.tile([P, PAIRS], F32, name="frac%d" % a)
+            fracs[a] = f
+            nc.vector.scalar_tensor_tensor(out=f[:, 0:REDUCED], in0=inv[:, 0:REDUCED], scalar=tcolumn, in1=ni[:],
+                                           op0=ALU.mult, op1=ALU.subtract)
+            nc.vector.tensor_scalar(out=f[:, REDUCED:PAIRS], in0=inv[:, REDUCED:PAIRS], scalar1=tcolumn, scalar2=None,
+                                    op0=ALU.mult)
+
+        def tables(a):
+            f = fracs[a]
+            tab = const.tile([P, 3, PAIRS], F32, name="tab%d" % a)
+            nc.scalar.activation(out=tab[:, 2, :], in_=f[:], func=ACT.Sin, scale=TWO_PI)
+            ag = tabtmp.tile([P, PAIRS], F32, name="ag")
+            nc.scalar.activation(out=ag[:], in_=f[:], func=ACT.Abs)
+            nc.scalar.activation(out=tab[:, 1, :], in_=ag[:], func=ACT.Sin, scale=-TWO_PI, bias=0.5 * math.pi)
+            nc.scalar.activation(out=tab[:, 0, :], in_=f[:], func=ACT.Sin, scale=-TWO_PI)
+            tabs[a] = tab
+
+        def transpose_words(src):
+            tp = tps.tile([P, 2 * PASSES, P], F32, name="tp")
+            words = src.bitcast(F32)
+            for g in range(PASSES):
+                for u in range(2):
+                    nc.tensor.transpose(tp[:, 2 * g + u, :], words[:, 256 * g + u:256 * (g + 1):2], ident[:])
+            return tp
+
+        xcodes, xscales = [], []
+        for a in range(POS_TILES):
+            xc_a = const.tile([P, B * PASSES * P], U32, name="xc%d" % a, align_bytes=64)
+            xs_a = const.tile([P, B * PASSES * P], U8, name="xs%d" % a, align_bytes=64)
+            xcodes.append(xc_a)
+            xscales.append(xs_a)
+
+        widened, grouped = {}, {}
+
+        def widen(b):
+            xw = xwp.tile([P, D], BF16, name="xw")
+            nc.vector.tensor_tensor(out=xw[:], in0=xbytes[0][:, b, :].bitcast(FP8), in1=xs_bc[:], op=ALU.mult)
+            widened[b] = xw
+
+        def turn_x(b):
+            tp = transpose_words(widened[b][:])
+            xg = xgp.tile([P, PASSES * P * 4], BF16, name="xg", align_bytes=64)
+            nc.scalar.copy(out=xg[:].bitcast(F32).rearrange("p (g r u) -> p g r u", g=PASSES, u=2),
+                           in_=tp[:].rearrange("p (g u) r -> p g r u", g=PASSES))
+            grouped[b] = xg
+
+        def quant_x(b):
+            cols = slice(b * PASSES * P, (b + 1) * PASSES * P)
+            nc.vector.quantize_mx(out=xcodes[0][:, cols].bitcast(FP8X4), scales=xscales[0][:, cols], in_=grouped[b][:])
+
+        casts, grouped4 = {}, {}
+
+        def cast_group(a, engine_copy):
+            xcast = xcp.tile([P, B, D], BF16, name="xcast")
+            for b in range(B):
+                engine_copy(out=xcast[:, b, :], in_=xbytes[a][:, b, :].bitcast(FP8))
+            casts[a] = xcast
+
+        def bank(a, k):
+            g, u = k // 2, k % 2
+            if k == 0:
+                xg4_new = xg4p.tile([P, B * PASSES * P * 4], BF16, name="xg4", align_bytes=64)
+                grouped4[a] = xg4_new
+            xg4v = grouped4[a][:].rearrange("p (b g r t) -> p b g r t", b=B, g=PASSES, t=4)
+            tp = tps.tile([P, B, P], F32, name="tp")
+            for b in range(B):
+                words = casts[a][:, b, :].bitcast(F32)
+                nc.tensor.transpose(tp[:, b, :], words[:, 256 * g + u:256 * (g + 1):2], ident[:])
+            halves = tp[:].rearrange("p b r -> p (b r)").bitcast(BF16).rearrange("p (b r e) -> p b r e", b=B, e=2)
+            for e in range(2):
+                t = 2 * u + e
+                nc.scalar.activation(out=xg4v[:, :, g, :, t], in_=halves[:, :, :, e], func=ACT.Copy,
+                                     scale=xs_col[:, g, t:t + 1])
+
+        def quant_group(a, half):
+            cols = slice(half * 2 * PASSES * P, (half + 1) * 2 * PASSES * P)
+            nc.vector.quantize_mx(out=xcodes[a][:, cols].bitcast(FP8X4), scales=xscales[a][:, cols],
+                                  in_=grouped4[a][:, 4 * cols.start:4 * cols.stop])
+
+        wcodes, wscales, wgrouped = {}, {}, {}
+
+        def turn_w(c):
+            wg = wgp.tile([P, PASSES * 512 * 4], BF16, name="wg", align_bytes=64)
+            wgrouped[c] = wg
+            wgw = wg[:].bitcast(F32).rearrange("p (g r u) -> p g r u", g=PASSES, u=2)
+            for r in range(4):
+                tp = transpose_words(wraw[c][:, r, :])
+                nc.scalar.copy(out=wgw[:, :, r * P:(r + 1) * P, :],
+                               in_=tp[:].rearrange("p (g u) r -> p g r u", g=PASSES))
+
+        def quant_w(c):
+            wc = const.tile([P, PASSES * 512], U32, name="wc%d" % c, align_bytes=64)
+            ws = const.tile([P, PASSES * 512], U8, name="ws%d" % c, align_bytes=64)
+            nc.vector.quantize_mx(out=wc[:].bitcast(FP8X4), scales=ws[:], in_=wgrouped[c][:])
+            wcodes[c] = wc
+            wscales[c] = ws
+
+        units = [(0, b, 0) for b in range(B)] + [(0, b, 1) for b in range(B)]
+        units += [(a, b, m) for a in range(1, POS_TILES) for b in range(B) for m in range(2)]
+        sums = {}
+
+        def project(a, b, c):
+            acc = accp.tile([P, 512], F32, name="acc")
+            for g in range(PASSES):
+                cols = slice((b * PASSES + g) * P, (b * PASSES + g + 1) * P)
+                nc.tensor.matmul_mx(
+                    out=acc[:],
+                    lhsT=xcodes[a][:, cols].bitcast(FP8X4),
+                    lhsT_scale=xscales[a][:, cols],
+                    rhs=wcodes[c][:, g * 512:(g + 1) * 512].bitcast(FP8X4),
+                    rhs_scale=wscales[c][:, g * 512:(g + 1) * 512],
+                    start=(g == 0),
+                    stop=(g == PASSES - 1),
+                )
+            return acc
+
+        def mm(j):
+            a, b, m = units[j]
+            even = project(a, b, 2 * m)
+            odd = project(a, b, 2 * m + 1)
+            sums[j] = (even, odd)
+
+        pair = {}
+
+        def vg(j, pieces=1):
+            a, b, m = units[j]
+            even, odd = sums[j]
+            if j % 2 == 0:
+                pt_new = pqp.tile([P, 2 * E], F32, name="pt")
+                qt_new = pqp.tile([P, 2 * E], F32, name="qt")
+                ot_new = op.tile([P, 2 * E], F32, name="ot")
+                pair["t"] = (pt_new, qt_new, ot_new)
+            pt, qt, ot = pair["t"]
+            base = (j % 2) * E
+            step = PAIRS // pieces
+            for h in range(pieces):
+                pr = slice(h * step, (h + 1) * step)
+                cols = slice(base + 2 * h * step, base + 2 * (h + 1) * step)
+                nc.vector.tensor_tensor(out=pt[:, cols].rearrange("p (i e) -> p i e", e=2),
+                                        in0=tabs[a][:, 1:3, pr].rearrange("p e i -> p i e"),
+                                        in1=even[:, pr].unsqueeze(2).to_broadcast([P, step, 2]), op=ALU.mult)
+                nc.vector.tensor_tensor(out=qt[:, cols].rearrange("p (i e) -> p i e", e=2),
+                                        in0=tabs[a][:, 0:2, pr].rearrange("p e i -> p i e"),
+                                        in1=odd[:, pr].unsqueeze(2).to_broadcast([P, step, 2]), op=ALU.mult)
+                if j >= len(units) - 2:
+                    nc.gpsimd.tensor_tensor(out=ot[:, cols], in0=pt[:, cols], in1=qt[:, cols], op=ALU.add)
+                    nc.sync.dma_start(out=outs[m][b, a * P:(a + 1) * P, cols.start - base:cols.stop - base],
+                                      in_=ot[:, cols])
+            if j % 2 == 1 and j < len(units) - 2:
+                nc.gpsimd.tensor_tensor(out=ot[:], in0=pt[:], in1=qt[:], op=ALU.add)
+                for jj in (j - 1, j):
+                    a2, b2, m2 = units[jj]
+                    nc.sync.dma_start(out=outs[m2][b2, a2 * P:(a2 + 1) * P, :],
+                                      in_=ot[:, (jj % 2) * E:(jj % 2 + 1) * E])
+
+        cast_group(1, nc.gpsimd.tensor_copy)
+        table_turns(0)
+        tables(0)
+        widen(0)
+        turn_x(0)
+        widen(1)
+        quant_x(0)
+        widen(2)
+        widen(3)
+        table_turns(1)
+        table_turns(2)
+        table_turns(3)
+        turn_w(0)
+        quant_w(0)
+        turn_w(1)
+        turn_x(1)
+        turn_x(2)
+        quant_w(1)
+        quant_x(1)
+        quant_x(2)
+        mm(0)
+        turn_x(3)
+        tables(1)
+        mm(1)
+        mm(2)
+        turn_w(2)
+        vg(0)
+        quant_x(3)
+        mm(3)
+        turn_w(3)
+        vg(1)
+        vg(2)
+        quant_w(2)
+        quant_w(3)
+        bank(1, 0)
+        bank(1, 1)
+        mm(4)
+        mm(5)
+        vg(3)
+        mm(6)
+        bank(1, 2)
+        vg(4)
+        mm(7)
+        bank(1, 3)
+        vg(5)
+        vg(6)
+        vg(7)
+        for a in range(1, POS_TILES):
+            first = 8 * a
+            quant_group(a, 0)
+            mm(first)
+            mm(first + 1)
+            mm(first + 2)
+            quant_group(a, 1)
+            for j in range(first, first + 8):
+                vg(j, 2 if j == len(units) - 1 else 1)
+                if j + 3 < first + 8:
+                    mm(j + 3)
+                if a + 1 < POS_TILES:
+                    if j + 3 == first + 3:
+                        cast_group(a + 1, nc.scalar.copy)
+                        tables(a + 1)
+                        bank(a + 1, 0)
+                        bank(a + 1, 1)
+                    if j + 3 == first + 6:
+                        bank(a + 1, 2)
+                    if j + 3 == first + 7:
+                        bank(a + 1, 3)

@@ -33,7 +33,7 @@ def tile_attention_pa_kernel(tc, x_bytes, x_scale, wq, wk, out_0, out_1):
 
     with ExitStack() as ctx:
         const = ctx.enter_context(tc.tile_pool(name="const", bufs=1))
-        tabtmp = ctx.enter_context(tc.tile_pool(name="tabtmp", bufs=2))
+        tabp = ctx.enter_context(tc.tile_pool(name="tabp", bufs=2))
         xwp = ctx.enter_context(tc.tile_pool(name="xwp", bufs=3))
         xgp = ctx.enter_context(tc.tile_pool(name="xgp", bufs=3))
         xcp = ctx.enter_context(tc.tile_pool(name="xcp", bufs=1))
@@ -90,29 +90,42 @@ def tile_attention_pa_kernel(tc, x_bytes, x_scale, wq, wk, out_0, out_1):
                                     scalar2=None, op0=ALU.mult)
             n *= 2
 
-        fracs = {}
+        args = {}
         tabs = {}
 
-        def table_turns(a):
-            tcolumn = turns[:, a:a + 1]
-            ni = tabtmp.tile([P, REDUCED], I32, name="ni")
-            nc.vector.tensor_scalar(out=ni[:], in0=inv[:, 0:REDUCED], scalar1=tcolumn, scalar2=None, op0=ALU.mult)
-            f = const.tile([P, PAIRS], F32, name="frac%d" % a)
-            fracs[a] = f
-            nc.vector.scalar_tensor_tensor(out=f[:, 0:REDUCED], in0=inv[:, 0:REDUCED], scalar=tcolumn, in1=ni[:],
-                                           op0=ALU.mult, op1=ALU.subtract)
-            nc.vector.tensor_scalar(out=f[:, REDUCED:PAIRS], in0=inv[:, REDUCED:PAIRS], scalar1=tcolumn, scalar2=None,
-                                    op0=ALU.mult)
+        def table_turns(group):
+            whole = {}
+            for a in group:
+                ni = const.tile([P, REDUCED], I32, name="ni%d" % a)
+                whole[a] = ni
+                nc.vector.tensor_scalar(out=ni[:], in0=inv[:, 0:REDUCED], scalar1=turns[:, a:a + 1], scalar2=None,
+                                        op0=ALU.mult)
+                arg_new = const.tile([P, 3, PAIRS], F32, name="arg%d" % a)
+                args[a] = arg_new
+            for a in group:
+                nc.vector.tensor_scalar(out=args[a][:, 2, REDUCED:PAIRS], in0=inv[:, REDUCED:PAIRS],
+                                        scalar1=turns[:, a:a + 1], scalar2=None, op0=ALU.mult)
+            for a in group:
+                nc.vector.scalar_tensor_tensor(out=args[a][:, 2, 0:REDUCED], in0=inv[:, 0:REDUCED],
+                                               scalar=turns[:, a:a + 1], in1=whole[a][:],
+                                               op0=ALU.mult, op1=ALU.subtract)
+            for a in group:
+                nc.vector.tensor_scalar(out=args[a][:, 0, :], in0=args[a][:, 2, :], scalar1=-1.0, scalar2=None,
+                                        op0=ALU.mult)
+            for a in group:
+                nc.vector.tensor_tensor(out=args[a][:, 1, :], in0=args[a][:, 2, :], in1=args[a][:, 0, :], op=ALU.min)
+            for a in group:
+                nc.vector.tensor_scalar(out=args[a][:, 1, :], in0=args[a][:, 1, :], scalar1=0.25, scalar2=None,
+                                        op0=ALU.add)
 
         def tables(a):
-            f = fracs[a]
-            tab = const.tile([P, 3, PAIRS], F32, name="tab%d" % a)
-            nc.scalar.activation(out=tab[:, 2, :], in_=f[:], func=ACT.Sin, scale=TWO_PI)
-            ag = tabtmp.tile([P, PAIRS], F32, name="ag")
-            nc.scalar.activation(out=ag[:], in_=f[:], func=ACT.Abs)
-            nc.scalar.activation(out=tab[:, 1, :], in_=ag[:], func=ACT.Sin, scale=-TWO_PI, bias=0.5 * math.pi)
-            nc.scalar.activation(out=tab[:, 0, :], in_=f[:], func=ACT.Sin, scale=-TWO_PI)
-            tabs[a] = tab
+            cs = tabp.tile([P, PAIRS, 2], F32, name="cs")
+            nsc = tabp.tile([P, PAIRS, 2], F32, name="nsc")
+            nc.scalar.activation(out=cs[:], in_=args[a][:, 1:3, :].rearrange("p e i -> p i e"), func=ACT.Sin,
+                                 scale=TWO_PI)
+            nc.scalar.activation(out=nsc[:], in_=args[a][:, 0:2, :].rearrange("p e i -> p i e"), func=ACT.Sin,
+                                 scale=TWO_PI)
+            tabs[a] = (cs, nsc)
 
         def transpose_words(src):
             tp = tps.tile([P, 2 * PASSES, P], F32, name="tp")
@@ -236,10 +249,10 @@ def tile_attention_pa_kernel(tc, x_bytes, x_scale, wq, wk, out_0, out_1):
                 pr = slice(h * step, (h + 1) * step)
                 cols = slice(base + 2 * h * step, base + 2 * (h + 1) * step)
                 nc.vector.tensor_tensor(out=pt[:, cols].rearrange("p (i e) -> p i e", e=2),
-                                        in0=tabs[a][:, 1:3, pr].rearrange("p e i -> p i e"),
+                                        in0=tabs[a][0][:, pr, :],
                                         in1=even[:, pr].unsqueeze(2).to_broadcast([P, step, 2]), op=ALU.mult)
                 nc.vector.tensor_tensor(out=qt[:, cols].rearrange("p (i e) -> p i e", e=2),
-                                        in0=tabs[a][:, 0:2, pr].rearrange("p e i -> p i e"),
+                                        in0=tabs[a][1][:, pr, :],
                                         in1=odd[:, pr].unsqueeze(2).to_broadcast([P, step, 2]), op=ALU.mult)
                 if j >= len(units) - 2:
                     nc.gpsimd.tensor_tensor(out=ot[:, cols], in0=pt[:, cols], in1=qt[:, cols], op=ALU.add)
@@ -253,7 +266,7 @@ def tile_attention_pa_kernel(tc, x_bytes, x_scale, wq, wk, out_0, out_1):
                                       in_=ot[:, (jj % 2) * E:(jj % 2 + 1) * E])
 
         cast_group(1, nc.gpsimd.tensor_copy)
-        table_turns(0)
+        table_turns([0])
         tables(0)
         widen(0)
         turn_x(0)
@@ -261,9 +274,7 @@ def tile_attention_pa_kernel(tc, x_bytes, x_scale, wq, wk, out_0, out_1):
         quant_x(0)
         widen(2)
         widen(3)
-        table_turns(1)
-        table_turns(2)
-        table_turns(3)
+        table_turns([1, 2, 3])
         turn_w(0)
         quant_w(0)
         turn_w(1)

@@ -33,15 +33,14 @@ def tile_attention_pa_kernel(tc, x_bytes, x_scale, wq, wk, out_0, out_1):
 
     with ExitStack() as ctx:
         const = ctx.enter_context(tc.tile_pool(name="const", bufs=1))
-        tabp = ctx.enter_context(tc.tile_pool(name="tabp", bufs=2))
+        tabp = ctx.enter_context(tc.tile_pool(name="tabp", bufs=4))
         xwp = ctx.enter_context(tc.tile_pool(name="xwp", bufs=3))
         xgp = ctx.enter_context(tc.tile_pool(name="xgp", bufs=3))
-        xcp = ctx.enter_context(tc.tile_pool(name="xcp", bufs=1))
+        xcp = ctx.enter_context(tc.tile_pool(name="xcp", bufs=2))
         xg4p = ctx.enter_context(tc.tile_pool(name="xg4p", bufs=1))
         wgp = ctx.enter_context(tc.tile_pool(name="wgp", bufs=2))
-        pqp = ctx.enter_context(tc.tile_pool(name="pqp", bufs=2))
         op = ctx.enter_context(tc.tile_pool(name="op", bufs=2))
-        wrp = ctx.enter_context(tc.tile_pool(name="wrp", bufs=4))
+        slabs = ctx.enter_context(tc.tile_pool(name="slabs", bufs=5))
         tps = ctx.enter_context(tc.psum_pool(name="tps", bufs=2))
         accp = ctx.enter_context(tc.psum_pool(name="accp", bufs=6))
         ctx.enter_context(tc.manual_schedule(engines={mybir.EngineType.PE, mybir.EngineType.DVE}))
@@ -62,14 +61,14 @@ def tile_attention_pa_kernel(tc, x_bytes, x_scale, wq, wk, out_0, out_1):
 
         def load_w(c):
             src = weights[c // 2].rearrange("(r p e) k -> e p r k", p=P, e=2)
-            wraw_c = wrp.tile([P, 4, D], BF16, name="wraw")
+            wraw_c = slabs.tile([P, 4, D], BF16, name="slab")
             wraw.append(wraw_c)
             nc.sync.dma_start(out=wraw_c[:], in_=src[c % 2])
 
         load_x(0)
         load_w(0)
-        load_w(1)
         load_x(1)
+        load_w(1)
         load_w(2)
         load_w(3)
         load_x(2)
@@ -168,6 +167,23 @@ def tile_attention_pa_kernel(tc, x_bytes, x_scale, wq, wk, out_0, out_1):
                 engine_copy(out=xcast[:, b, :], in_=xbytes[a][:, b, :].bitcast(FP8))
             casts[a] = xcast
 
+        def widen4(a, b):
+            if b == 0:
+                xcast = xcp.tile([P, B, D], BF16, name="xcast")
+                casts[a] = xcast
+            nc.vector.tensor_tensor(out=casts[a][:, b, :], in0=xbytes[a][:, b, :].bitcast(FP8), in1=xs_bc[:],
+                                    op=ALU.mult)
+
+        def turn_x4(a, b):
+            if b == 0:
+                xg4_new = xg4p.tile([P, B * PASSES * P * 4], BF16, name="xg4", align_bytes=64)
+                grouped4[a] = xg4_new
+            tp = transpose_words(casts[a][:, b, :])
+            width = PASSES * P * 4
+            nc.scalar.copy(out=grouped4[a][:, b * width:(b + 1) * width].bitcast(F32)
+                           .rearrange("p (g r u) -> p g r u", g=PASSES, u=2),
+                           in_=tp[:].rearrange("p (g u) r -> p g r u", g=PASSES))
+
         def bank(a, k):
             g, u = k // 2, k % 2
             if k == 0:
@@ -238,8 +254,8 @@ def tile_attention_pa_kernel(tc, x_bytes, x_scale, wq, wk, out_0, out_1):
             a, b, m = units[j]
             even, odd = sums[j]
             if j % 2 == 0:
-                pt_new = pqp.tile([P, 2 * E], F32, name="pt")
-                qt_new = pqp.tile([P, 2 * E], F32, name="qt")
+                pt_new = slabs.tile([P, 2 * E], F32, name="slab")
+                qt_new = slabs.tile([P, 2 * E], F32, name="slab")
                 ot_new = op.tile([P, 2 * E], F32, name="ot")
                 pair["t"] = (pt_new, qt_new, ot_new)
             pt, qt, ot = pair["t"]
@@ -265,7 +281,7 @@ def tile_attention_pa_kernel(tc, x_bytes, x_scale, wq, wk, out_0, out_1):
                     nc.sync.dma_start(out=outs[m2][b2, a2 * P:(a2 + 1) * P, :],
                                       in_=ot[:, (jj % 2) * E:(jj % 2 + 1) * E])
 
-        cast_group(1, nc.gpsimd.tensor_copy)
+        cast_group(2, nc.gpsimd.tensor_copy)
         table_turns([0])
         tables(0)
         widen(0)
@@ -275,8 +291,12 @@ def tile_attention_pa_kernel(tc, x_bytes, x_scale, wq, wk, out_0, out_1):
         widen(2)
         widen(3)
         table_turns([1, 2, 3])
+        widen4(1, 0)
+        widen4(1, 1)
         turn_w(0)
         quant_w(0)
+        widen4(1, 2)
+        widen4(1, 3)
         turn_w(1)
         turn_x(1)
         turn_x(2)
@@ -293,20 +313,23 @@ def tile_attention_pa_kernel(tc, x_bytes, x_scale, wq, wk, out_0, out_1):
         quant_x(3)
         mm(3)
         turn_w(3)
+        tables(2)
+        tables(3)
         vg(1)
         vg(2)
         quant_w(2)
         quant_w(3)
-        bank(1, 0)
-        bank(1, 1)
+        turn_x4(1, 0)
+        turn_x4(1, 1)
         mm(4)
         mm(5)
         vg(3)
         mm(6)
-        bank(1, 2)
+        turn_x4(1, 2)
         vg(4)
         mm(7)
-        bank(1, 3)
+        turn_x4(1, 3)
+        cast_group(3, nc.scalar.copy)
         vg(5)
         vg(6)
         vg(7)
@@ -323,8 +346,6 @@ def tile_attention_pa_kernel(tc, x_bytes, x_scale, wq, wk, out_0, out_1):
                     mm(j + 3)
                 if a + 1 < POS_TILES:
                     if j + 3 == first + 3:
-                        cast_group(a + 1, nc.scalar.copy)
-                        tables(a + 1)
                         bank(a + 1, 0)
                         bank(a + 1, 1)
                     if j + 3 == first + 6:

@@ -39,8 +39,7 @@ def tile_attention_pa_kernel(tc, x_bytes, x_scale, wq, wk, out_0, out_1):
         xcp = ctx.enter_context(tc.tile_pool(name="xcp", bufs=2))
         xg4p = ctx.enter_context(tc.tile_pool(name="xg4p", bufs=1))
         wgp = ctx.enter_context(tc.tile_pool(name="wgp", bufs=2))
-        op = ctx.enter_context(tc.tile_pool(name="op", bufs=2))
-        slabs = ctx.enter_context(tc.tile_pool(name="slabs", bufs=5))
+        slabs = ctx.enter_context(tc.tile_pool(name="slabs", bufs=7))
         tps = ctx.enter_context(tc.psum_pool(name="tps", bufs=2))
         accp = ctx.enter_context(tc.psum_pool(name="accp", bufs=6))
         ctx.enter_context(tc.manual_schedule(engines={mybir.EngineType.PE, mybir.EngineType.DVE}))
@@ -256,9 +255,8 @@ def tile_attention_pa_kernel(tc, x_bytes, x_scale, wq, wk, out_0, out_1):
             if j % 2 == 0:
                 pt_new = slabs.tile([P, 2 * E], F32, name="slab")
                 qt_new = slabs.tile([P, 2 * E], F32, name="slab")
-                ot_new = op.tile([P, 2 * E], F32, name="ot")
-                pair["t"] = (pt_new, qt_new, ot_new)
-            pt, qt, ot = pair["t"]
+                pair["t"] = (pt_new, qt_new)
+            pt, qt = pair["t"]
             base = (j % 2) * E
             step = PAIRS // pieces
             for h in range(pieces):
@@ -271,15 +269,15 @@ def tile_attention_pa_kernel(tc, x_bytes, x_scale, wq, wk, out_0, out_1):
                                         in0=tabs[a][1][:, pr, :],
                                         in1=odd[:, pr].unsqueeze(2).to_broadcast([P, step, 2]), op=ALU.mult)
                 if j >= len(units) - 2:
-                    nc.gpsimd.tensor_tensor(out=ot[:, cols], in0=pt[:, cols], in1=qt[:, cols], op=ALU.add)
+                    nc.gpsimd.tensor_tensor(out=pt[:, cols], in0=pt[:, cols], in1=qt[:, cols], op=ALU.add)
                     nc.sync.dma_start(out=outs[m][b, a * P:(a + 1) * P, cols.start - base:cols.stop - base],
-                                      in_=ot[:, cols])
+                                      in_=pt[:, cols])
             if j % 2 == 1 and j < len(units) - 2:
-                nc.gpsimd.tensor_tensor(out=ot[:], in0=pt[:], in1=qt[:], op=ALU.add)
+                nc.gpsimd.tensor_tensor(out=pt[:], in0=pt[:], in1=qt[:], op=ALU.add)
                 for jj in (j - 1, j):
                     a2, b2, m2 = units[jj]
                     nc.sync.dma_start(out=outs[m2][b2, a2 * P:(a2 + 1) * P, :],
-                                      in_=ot[:, (jj % 2) * E:(jj % 2 + 1) * E])
+                                      in_=pt[:, (jj % 2) * E:(jj % 2 + 1) * E])
 
         cast_group(2, nc.gpsimd.tensor_copy)
         table_turns([0])

@@ -24,6 +24,7 @@ POS_TILES = S // P
 PASSES = D // 512
 TWO_PI = 2.0 * math.pi
 REDUCED = 288
+VECTOR_ADDS_EVERY = 8
 
 
 def tile_attention_pa_kernel(tc, x_bytes, x_scale, wq, wk, out_0, out_1):
@@ -248,6 +249,20 @@ def tile_attention_pa_kernel(tc, x_bytes, x_scale, wq, wk, out_0, out_1):
             sums[j] = (even, odd)
 
         pair = {}
+        waiting = []
+
+        def store(j, tile_ap, first_col, last_col):
+            a, b, m = units[j]
+            nc.sync.dma_start(out=outs[m][b, a * P:(a + 1) * P, first_col:last_col], in_=tile_ap)
+
+        def vector_adds():
+            for j, pt, qt, cols, base in waiting:
+                nc.vector.tensor_tensor(out=pt[:, cols], in0=pt[:, cols], in1=qt[:, cols], op=ALU.add)
+                store(j, pt[:, cols], cols.start - base, cols.stop - base)
+            waiting.clear()
+
+        def by_vector(j):
+            return j % VECTOR_ADDS_EVERY == VECTOR_ADDS_EVERY - 1
 
         def vg(j, pieces=1):
             a, b, m = units[j]
@@ -265,19 +280,20 @@ def tile_attention_pa_kernel(tc, x_bytes, x_scale, wq, wk, out_0, out_1):
                 nc.vector.tensor_tensor(out=pt[:, cols].rearrange("p (i e) -> p i e", e=2),
                                         in0=tabs[a][0][:, pr, :],
                                         in1=even[:, pr].unsqueeze(2).to_broadcast([P, step, 2]), op=ALU.mult)
+                if j % 2 == 0:
+                    vector_adds()
                 nc.vector.tensor_tensor(out=qt[:, cols].rearrange("p (i e) -> p i e", e=2),
                                         in0=tabs[a][1][:, pr, :],
                                         in1=odd[:, pr].unsqueeze(2).to_broadcast([P, step, 2]), op=ALU.mult)
-                if j >= len(units) - 2:
-                    nc.gpsimd.tensor_tensor(out=pt[:, cols], in0=pt[:, cols], in1=qt[:, cols], op=ALU.add)
-                    nc.sync.dma_start(out=outs[m][b, a * P:(a + 1) * P, cols.start - base:cols.stop - base],
-                                      in_=pt[:, cols])
-            if j % 2 == 1 and j < len(units) - 2:
+                if by_vector(j):
+                    waiting.append((j, pt, qt, cols, base))
+            if j % 2 == 0 and by_vector(j + 1):
+                nc.gpsimd.tensor_tensor(out=pt[:, 0:E], in0=pt[:, 0:E], in1=qt[:, 0:E], op=ALU.add)
+                store(j, pt[:, 0:E], 0, E)
+            if j % 2 == 1 and not by_vector(j):
                 nc.gpsimd.tensor_tensor(out=pt[:], in0=pt[:], in1=qt[:], op=ALU.add)
-                for jj in (j - 1, j):
-                    a2, b2, m2 = units[jj]
-                    nc.sync.dma_start(out=outs[m2][b2, a2 * P:(a2 + 1) * P, :],
-                                      in_=pt[:, (jj % 2) * E:(jj % 2 + 1) * E])
+                store(j - 1, pt[:, 0:E], 0, E)
+                store(j, pt[:, E:2 * E], 0, E)
 
         cast_group(2, nc.gpsimd.tensor_copy)
         table_turns([0])
@@ -350,3 +366,4 @@ def tile_attention_pa_kernel(tc, x_bytes, x_scale, wq, wk, out_0, out_1):
                         bank(a + 1, 2)
                     if j + 3 == first + 7:
                         bank(a + 1, 3)
+        vector_adds()

@@ -39,8 +39,9 @@ def tile_attention_pa_kernel(tc, x_bytes, x_scale, wq, wk, out_0, out_1):
         xgp = ctx.enter_context(tc.tile_pool(name="xgp", bufs=3))
         xcp = ctx.enter_context(tc.tile_pool(name="xcp", bufs=2))
         xg4p = ctx.enter_context(tc.tile_pool(name="xg4p", bufs=1))
+        xplp = ctx.enter_context(tc.tile_pool(name="xplp", bufs=1))
         wgp = ctx.enter_context(tc.tile_pool(name="wgp", bufs=2))
-        slabs = ctx.enter_context(tc.tile_pool(name="slabs", bufs=7))
+        slabs = ctx.enter_context(tc.tile_pool(name="slabs", bufs=6))
         tps = ctx.enter_context(tc.psum_pool(name="tps", bufs=2))
         accp = ctx.enter_context(tc.psum_pool(name="accp", bufs=6))
         ctx.enter_context(tc.manual_schedule(engines={mybir.EngineType.PE, mybir.EngineType.DVE}))
@@ -108,14 +109,18 @@ def tile_attention_pa_kernel(tc, x_bytes, x_scale, wq, wk, out_0, out_1):
                 nc.vector.scalar_tensor_tensor(out=args[a][:, 2, 0:REDUCED], in0=inv[:, 0:REDUCED],
                                                scalar=turns[:, a:a + 1], in1=whole[a][:],
                                                op0=ALU.mult, op1=ALU.subtract)
-            for a in group:
-                nc.vector.tensor_scalar(out=args[a][:, 0, :], in0=args[a][:, 2, :], scalar1=-1.0, scalar2=None,
-                                        op0=ALU.mult)
-            for a in group:
-                nc.vector.tensor_tensor(out=args[a][:, 1, :], in0=args[a][:, 2, :], in1=args[a][:, 0, :], op=ALU.min)
-            for a in group:
-                nc.vector.tensor_scalar(out=args[a][:, 1, :], in0=args[a][:, 1, :], scalar1=0.25, scalar2=None,
-                                        op0=ALU.add)
+
+        def planes_on_vector(a):
+            nc.vector.tensor_scalar(out=args[a][:, 0, :], in0=args[a][:, 2, :], scalar1=-1.0, scalar2=None,
+                                    op0=ALU.mult)
+            nc.vector.tensor_tensor(out=args[a][:, 1, :], in0=args[a][:, 2, :], in1=args[a][:, 0, :], op=ALU.min)
+            nc.vector.tensor_scalar(out=args[a][:, 1, :], in0=args[a][:, 1, :], scalar1=0.25, scalar2=None,
+                                    op0=ALU.add)
+
+        def planes_on_scalar(a):
+            nc.scalar.activation(out=args[a][:, 0, :], in_=args[a][:, 2, :], func=ACT.Copy, scale=-1.0)
+            nc.scalar.activation(out=args[a][:, 1, :], in_=args[a][:, 2, :], func=ACT.Abs)
+            nc.scalar.activation(out=args[a][:, 1, :], in_=args[a][:, 1, :], func=ACT.Identity, scale=-1.0, bias=0.25)
 
         def tables(a):
             cs = tabp.tile([P, PAIRS, 2], F32, name="cs")
@@ -184,12 +189,13 @@ def tile_attention_pa_kernel(tc, x_bytes, x_scale, wq, wk, out_0, out_1):
                            .rearrange("p (g r u) -> p g r u", g=PASSES, u=2),
                            in_=tp[:].rearrange("p (g u) r -> p g r u", g=PASSES))
 
+        planes = {}
+
         def bank(a, k):
             g, u = k // 2, k % 2
             if k == 0:
-                xg4_new = xg4p.tile([P, B * PASSES * P * 4], BF16, name="xg4", align_bytes=64)
-                grouped4[a] = xg4_new
-            xg4v = grouped4[a][:].rearrange("p (b g r t) -> p b g r t", b=B, g=PASSES, t=4)
+                planes_new = xplp.tile([P, PASSES, 4, B * P], BF16, name="xpl")
+                planes[a] = planes_new
             tp = tps.tile([P, B, P], F32, name="tp")
             for b in range(B):
                 words = casts[a][:, b, :].bitcast(F32)
@@ -197,8 +203,15 @@ def tile_attention_pa_kernel(tc, x_bytes, x_scale, wq, wk, out_0, out_1):
             halves = tp[:].rearrange("p b r -> p (b r)").bitcast(BF16).rearrange("p (b r e) -> p b r e", b=B, e=2)
             for e in range(2):
                 t = 2 * u + e
-                nc.scalar.activation(out=xg4v[:, :, g, :, t], in_=halves[:, :, :, e], func=ACT.Copy,
-                                     scale=xs_col[:, g, t:t + 1])
+                nc.scalar.activation(out=planes[a][:, g, t, :].rearrange("p (b r) -> p b r", b=B),
+                                     in_=halves[:, :, :, e], func=ACT.Copy, scale=xs_col[:, g, t:t + 1])
+            if u == 1:
+                if g == 0:
+                    xg4_new = xg4p.tile([P, B * PASSES * P * 4], BF16, name="xg4", align_bytes=64)
+                    grouped4[a] = xg4_new
+                xg4v = grouped4[a][:].rearrange("p (b g r t) -> p b g r t", b=B, g=PASSES, t=4)
+                nc.scalar.copy(out=xg4v[:, :, g, :, :],
+                               in_=planes[a][:, g, :, :].rearrange("p t (b r) -> p b r t", b=B))
 
         def quant_group(a, half):
             cols = slice(half * 2 * PASSES * P, (half + 1) * 2 * PASSES * P)
@@ -295,8 +308,10 @@ def tile_attention_pa_kernel(tc, x_bytes, x_scale, wq, wk, out_0, out_1):
                 store(j - 1, pt[:, 0:E], 0, E)
                 store(j, pt[:, E:2 * E], 0, E)
 
+        cast_group(1, nc.gpsimd.tensor_copy)
         cast_group(2, nc.gpsimd.tensor_copy)
         table_turns([0])
+        planes_on_vector(0)
         tables(0)
         widen(0)
         turn_x(0)
@@ -305,12 +320,8 @@ def tile_attention_pa_kernel(tc, x_bytes, x_scale, wq, wk, out_0, out_1):
         widen(2)
         widen(3)
         table_turns([1, 2, 3])
-        widen4(1, 0)
-        widen4(1, 1)
         turn_w(0)
         quant_w(0)
-        widen4(1, 2)
-        widen4(1, 3)
         turn_w(1)
         turn_x(1)
         turn_x(2)
@@ -319,6 +330,7 @@ def tile_attention_pa_kernel(tc, x_bytes, x_scale, wq, wk, out_0, out_1):
         quant_x(2)
         mm(0)
         turn_x(3)
+        planes_on_scalar(1)
         tables(1)
         mm(1)
         mm(2)
@@ -327,23 +339,25 @@ def tile_attention_pa_kernel(tc, x_bytes, x_scale, wq, wk, out_0, out_1):
         quant_x(3)
         mm(3)
         turn_w(3)
-        tables(2)
-        tables(3)
         vg(1)
         vg(2)
         quant_w(2)
         quant_w(3)
-        turn_x4(1, 0)
-        turn_x4(1, 1)
+        bank(1, 0)
+        bank(1, 1)
         mm(4)
         mm(5)
         vg(3)
         mm(6)
-        turn_x4(1, 2)
+        bank(1, 2)
         vg(4)
         mm(7)
-        turn_x4(1, 3)
+        bank(1, 3)
         cast_group(3, nc.scalar.copy)
+        planes_on_scalar(2)
+        tables(2)
+        planes_on_scalar(3)
+        tables(3)
         vg(5)
         vg(6)
         vg(7)

@@ -300,13 +300,10 @@ def tile_attention_pa_kernel(tc, x_bytes, x_scale, wq, wk, out_0, out_1):
                                         in1=odd[:, pr].unsqueeze(2).to_broadcast([P, step, 2]), op=ALU.mult)
                 if by_vector(j):
                     waiting.append((j, pt, qt, cols, base))
-            if j % 2 == 0 and by_vector(j + 1):
-                nc.gpsimd.tensor_tensor(out=pt[:, 0:E], in0=pt[:, 0:E], in1=qt[:, 0:E], op=ALU.add)
-                store(j, pt[:, 0:E], 0, E)
-            if j % 2 == 1 and not by_vector(j):
-                nc.gpsimd.tensor_tensor(out=pt[:], in0=pt[:], in1=qt[:], op=ALU.add)
-                store(j - 1, pt[:, 0:E], 0, E)
-                store(j, pt[:, E:2 * E], 0, E)
+            if not by_vector(j):
+                nc.gpsimd.tensor_tensor(out=pt[:, base:base + E], in0=pt[:, base:base + E], in1=qt[:, base:base + E],
+                                        op=ALU.add)
+                store(j, pt[:, base:base + E], 0, E)
 
         cast_group(1, nc.gpsimd.tensor_copy)
         cast_group(2, nc.gpsimd.tensor_copy)
@@ -361,23 +358,30 @@ def tile_attention_pa_kernel(tc, x_bytes, x_scale, wq, wk, out_0, out_1):
         vg(5)
         vg(6)
         vg(7)
-        for a in range(1, POS_TILES):
-            first = 8 * a
-            quant_group(a, 0)
-            mm(first)
-            mm(first + 1)
-            mm(first + 2)
-            quant_group(a, 1)
-            for j in range(first, first + 8):
-                vg(j, 2 if j == len(units) - 1 else 1)
-                if j + 3 < first + 8:
-                    mm(j + 3)
-                if a + 1 < POS_TILES:
-                    if j + 3 == first + 3:
-                        bank(a + 1, 0)
-                        bank(a + 1, 1)
-                    if j + 3 == first + 6:
-                        bank(a + 1, 2)
-                    if j + 3 == first + 7:
-                        bank(a + 1, 3)
+        quant_group(1, 0)
+        mm(8)
+        mm(9)
+        mm(10)
+        quant_group(1, 1)
+        bank(2, 0)
+        bank(2, 1)
+        for j in range(8, len(units)):
+            if j in (13, 21):
+                quant_group(j // 8 + 1, 0)
+            if j in (14, 22):
+                quant_group(j // 8 + 1, 1)
+            vg(j, 2 if j == len(units) - 1 else 1)
+            if 10 < j + 3 < len(units):
+                mm(j + 3)
+            if j == 8:
+                bank(2, 2)
+            if j == 9:
+                bank(2, 3)
+            if j == 15:
+                bank(3, 0)
+                bank(3, 1)
+            if j == 16:
+                bank(3, 2)
+            if j == 17:
+                bank(3, 3)
         vector_adds()

@@ -20,11 +20,13 @@ ACT = mybir.ActivationFunctionType
 
 P = 128
 PAIRS = E // 2
+HALF = PAIRS // 2
 POS_TILES = S // P
 PASSES = D // 512
 TWO_PI = 2.0 * math.pi
 REDUCED = 288
-VECTOR_ADDS_EVERY = 8
+AHEAD = 4
+LATE = 2
 
 
 def tile_attention_pa_kernel(tc, x_bytes, x_scale, wq, wk, out_0, out_1):
@@ -35,19 +37,19 @@ def tile_attention_pa_kernel(tc, x_bytes, x_scale, wq, wk, out_0, out_1):
     with ExitStack() as ctx:
         const = ctx.enter_context(tc.tile_pool(name="const", bufs=1))
         tabp = ctx.enter_context(tc.tile_pool(name="tabp", bufs=4))
+        argp = ctx.enter_context(tc.tile_pool(name="argp", bufs=3))
         xwp = ctx.enter_context(tc.tile_pool(name="xwp", bufs=3))
         xgp = ctx.enter_context(tc.tile_pool(name="xgp", bufs=3))
         xcp = ctx.enter_context(tc.tile_pool(name="xcp", bufs=2))
         xg4p = ctx.enter_context(tc.tile_pool(name="xg4p", bufs=1))
         xplp = ctx.enter_context(tc.tile_pool(name="xplp", bufs=1))
         wgp = ctx.enter_context(tc.tile_pool(name="wgp", bufs=2))
-        slabs = ctx.enter_context(tc.tile_pool(name="slabs", bufs=6))
-        tps = ctx.enter_context(tc.psum_pool(name="tps", bufs=2))
-        accp = ctx.enter_context(tc.psum_pool(name="accp", bufs=6))
-        ctx.enter_context(tc.manual_schedule(engines={mybir.EngineType.PE, mybir.EngineType.DVE}))
+        slabs = ctx.enter_context(tc.tile_pool(name="slabs", bufs=7))
+        tps = ctx.enter_context(tc.psum_pool(name="tps", bufs=3))
+        accp = ctx.enter_context(tc.psum_pool(name="accp", bufs=5))
+        ctx.enter_context(tc.manual_schedule(engines={mybir.EngineType.PE, mybir.EngineType.DVE,
+                                                      mybir.EngineType.Activation, mybir.EngineType.Pool}))
 
-        xs_bc = const.tile([P, D], F32, name="xs_bc")
-        nc.sync.dma_start(out=xs_bc[:], in_=x_scale.rearrange("a b k -> (a b k)").partition_broadcast(P))
         xs_col = const.tile([P, PASSES, 4], F32, name="xs_col")
         nc.sync.dma_start(out=xs_col[:], in_=x_scale.rearrange("a b k -> (a b k)").rearrange("(g p t) -> p g t", p=P, t=4))
         xb_view = x_bytes.rearrange("b (a p) k -> a p b k", p=P)
@@ -61,13 +63,13 @@ def tile_attention_pa_kernel(tc, x_bytes, x_scale, wq, wk, out_0, out_1):
             nc.sync.dma_start(out=xbytes[a][:], in_=xb_view[a])
 
         def load_w(c):
-            src = weights[c // 2].rearrange("(r p e) k -> e p r k", p=P, e=2)
-            wraw_c = slabs.tile([P, 4, D], BF16, name="slab")
+            src = weights[c // 2].rearrange("(h v p z) k -> h p v z k", h=2, v=2, z=2)
+            wraw_c = slabs.tile([P, 2, 2, D], BF16, name="slab")
             wraw.append(wraw_c)
             nc.sync.dma_start(out=wraw_c[:], in_=src[c % 2])
 
-        load_x(0)
         load_w(0)
+        load_x(0)
         load_x(1)
         load_w(1)
         load_w(2)
@@ -75,40 +77,36 @@ def tile_attention_pa_kernel(tc, x_bytes, x_scale, wq, wk, out_0, out_1):
         load_x(2)
         load_x(3)
 
-        ident = const.tile([P, P], F32, name="ident")
-        make_identity(nc, ident[:])
         tcol = const.tile([P, POS_TILES], F32, name="tcol")
         nc.gpsimd.iota(tcol[:], pattern=[[P, POS_TILES]], base=0, channel_multiplier=1,
                        allow_small_or_imprecise_dtypes=True)
-        turns = const.tile([P, POS_TILES], F32, name="turns")
-        nc.vector.tensor_scalar(out=turns[:], in0=tcol[:], scalar1=1.0 / TWO_PI, scalar2=None, op0=ALU.mult)
+        ident = const.tile([P, P], F32, name="ident")
+        make_identity(nc, ident[:])
         inv = const.tile([P, PAIRS], F32, name="inv")
         nc.vector.memset(inv[:, 0:1], 1.0)
+        first_sin = const.tile([P, 1], F32, name="first_sin")
+        nc.scalar.activation(out=first_sin[:], in_=inv[:, 0:1], func=ACT.Sin)
         n = 1
         while n < PAIRS:
             nc.vector.tensor_scalar(out=inv[:, n:2 * n], in0=inv[:, 0:n], scalar1=THETA ** (-n / float(PAIRS)),
                                     scalar2=None, op0=ALU.mult)
             n *= 2
+        turns = const.tile([P, POS_TILES], F32, name="turns")
+        nc.vector.tensor_scalar(out=turns[:], in0=tcol[:], scalar1=1.0 / TWO_PI, scalar2=None, op0=ALU.mult)
 
         args = {}
         tabs = {}
 
-        def table_turns(group):
-            whole = {}
-            for a in group:
-                ni = const.tile([P, REDUCED], I32, name="ni%d" % a)
-                whole[a] = ni
-                nc.vector.tensor_scalar(out=ni[:], in0=inv[:, 0:REDUCED], scalar1=turns[:, a:a + 1], scalar2=None,
-                                        op0=ALU.mult)
-                arg_new = const.tile([P, 3, PAIRS], F32, name="arg%d" % a)
-                args[a] = arg_new
-            for a in group:
-                nc.vector.tensor_scalar(out=args[a][:, 2, REDUCED:PAIRS], in0=inv[:, REDUCED:PAIRS],
-                                        scalar1=turns[:, a:a + 1], scalar2=None, op0=ALU.mult)
-            for a in group:
-                nc.vector.scalar_tensor_tensor(out=args[a][:, 2, 0:REDUCED], in0=inv[:, 0:REDUCED],
-                                               scalar=turns[:, a:a + 1], in1=whole[a][:],
-                                               op0=ALU.mult, op1=ALU.subtract)
+        def table_turns(a):
+            whole = const.tile([P, REDUCED], I32, name="ni%d" % a)
+            arg_new = argp.tile([P, 3, PAIRS], F32, name="arg")
+            args[a] = arg_new
+            nc.vector.tensor_scalar(out=whole[:], in0=inv[:, 0:REDUCED], scalar1=turns[:, a:a + 1], scalar2=None,
+                                    op0=ALU.mult)
+            nc.vector.tensor_scalar(out=args[a][:, 2, REDUCED:PAIRS], in0=inv[:, REDUCED:PAIRS],
+                                    scalar1=turns[:, a:a + 1], scalar2=None, op0=ALU.mult)
+            nc.vector.scalar_tensor_tensor(out=args[a][:, 2, 0:REDUCED], in0=inv[:, 0:REDUCED],
+                                           scalar=turns[:, a:a + 1], in1=whole[:], op0=ALU.mult, op1=ALU.subtract)
 
         def planes_on_vector(a):
             nc.vector.tensor_scalar(out=args[a][:, 0, :], in0=args[a][:, 2, :], scalar1=-1.0, scalar2=None,
@@ -123,13 +121,21 @@ def tile_attention_pa_kernel(tc, x_bytes, x_scale, wq, wk, out_0, out_1):
             nc.scalar.activation(out=args[a][:, 1, :], in_=args[a][:, 1, :], func=ACT.Identity, scale=-1.0, bias=0.25)
 
         def tables(a):
-            cs = tabp.tile([P, PAIRS, 2], F32, name="cs")
-            nsc = tabp.tile([P, PAIRS, 2], F32, name="nsc")
-            nc.scalar.activation(out=cs[:], in_=args[a][:, 1:3, :].rearrange("p e i -> p i e"), func=ACT.Sin,
+            tab = tabp.tile([P, 2, PAIRS, 2], F32, name="tab")
+            nc.scalar.activation(out=tab[:, 0, :, :], in_=args[a][:, 1:3, :].rearrange("p e i -> p i e"), func=ACT.Sin,
                                  scale=TWO_PI)
-            nc.scalar.activation(out=nsc[:], in_=args[a][:, 0:2, :].rearrange("p e i -> p i e"), func=ACT.Sin,
+            nc.scalar.activation(out=tab[:, 1, :, :], in_=args[a][:, 0:2, :].rearrange("p e i -> p i e"), func=ACT.Sin,
                                  scale=TWO_PI)
-            tabs[a] = (cs, nsc)
+            tabs[a] = tab
+
+        xs_bc = const.tile([P, D], F32, name="xs_bc")
+
+        def spread_scales(g):
+            tp = tps.tile([P, 4, P], F32, name="tp")
+            for t in range(4):
+                nc.tensor.transpose(tp[:, t, :], xs_col[:, g, t:t + 1].to_broadcast([P, P]), ident[:])
+            nc.vector.tensor_copy(out=xs_bc[:, 512 * g:512 * (g + 1)].rearrange("p (n t) -> p n t", t=4),
+                                  in_=tp[:].rearrange("p t n -> p n t"))
 
         def transpose_words(src):
             tp = tps.tile([P, 2 * PASSES, P], F32, name="tp")
@@ -172,23 +178,6 @@ def tile_attention_pa_kernel(tc, x_bytes, x_scale, wq, wk, out_0, out_1):
                 engine_copy(out=xcast[:, b, :], in_=xbytes[a][:, b, :].bitcast(FP8))
             casts[a] = xcast
 
-        def widen4(a, b):
-            if b == 0:
-                xcast = xcp.tile([P, B, D], BF16, name="xcast")
-                casts[a] = xcast
-            nc.vector.tensor_tensor(out=casts[a][:, b, :], in0=xbytes[a][:, b, :].bitcast(FP8), in1=xs_bc[:],
-                                    op=ALU.mult)
-
-        def turn_x4(a, b):
-            if b == 0:
-                xg4_new = xg4p.tile([P, B * PASSES * P * 4], BF16, name="xg4", align_bytes=64)
-                grouped4[a] = xg4_new
-            tp = transpose_words(casts[a][:, b, :])
-            width = PASSES * P * 4
-            nc.scalar.copy(out=grouped4[a][:, b * width:(b + 1) * width].bitcast(F32)
-                           .rearrange("p (g r u) -> p g r u", g=PASSES, u=2),
-                           in_=tp[:].rearrange("p (g u) r -> p g r u", g=PASSES))
-
         planes = {}
 
         def bank(a, k):
@@ -220,14 +209,15 @@ def tile_attention_pa_kernel(tc, x_bytes, x_scale, wq, wk, out_0, out_1):
 
         wcodes, wscales, wgrouped = {}, {}, {}
 
-        def turn_w(c):
-            wg = wgp.tile([P, PASSES * 512 * 4], BF16, name="wg", align_bytes=64)
-            wgrouped[c] = wg
-            wgw = wg[:].bitcast(F32).rearrange("p (g r u) -> p g r u", g=PASSES, u=2)
-            for r in range(4):
-                tp = transpose_words(wraw[c][:, r, :])
-                nc.scalar.copy(out=wgw[:, :, r * P:(r + 1) * P, :],
-                               in_=tp[:].rearrange("p (g u) r -> p g r u", g=PASSES))
+        def turn_w(c, r, engine_copy):
+            if r == 0:
+                wg_new = wgp.tile([P, PASSES * 512 * 4], BF16, name="wg", align_bytes=64)
+                wgrouped[c] = wg_new
+            z, v = r // 2, r % 2
+            tp = transpose_words(wraw[c][:, v, z, :])
+            engine_copy(out=wgrouped[c][:].bitcast(F32).rearrange("p (g r u) -> p g r u", g=PASSES, u=2)
+                        [:, :, r * P:(r + 1) * P, :],
+                        in_=tp[:].rearrange("p (g u) r -> p g r u", g=PASSES))
 
         def quant_w(c):
             wc = const.tile([P, PASSES * 512], U32, name="wc%d" % c, align_bytes=64)
@@ -236,11 +226,12 @@ def tile_attention_pa_kernel(tc, x_bytes, x_scale, wq, wk, out_0, out_1):
             wcodes[c] = wc
             wscales[c] = ws
 
-        units = [(0, b, 0) for b in range(B)] + [(0, b, 1) for b in range(B)]
-        units += [(a, b, m) for a in range(1, POS_TILES) for b in range(B) for m in range(2)]
-        sums = {}
+        pieces = [(0, b, c) for c in range(4) for b in range(B)]
+        pieces += [(a, b, c) for a in range(1, POS_TILES) for b in range(B) for c in range(4)]
+        banks = {}
 
-        def project(a, b, c):
+        def mm(j):
+            a, b, c = pieces[j]
             acc = accp.tile([P, 512], F32, name="acc")
             for g in range(PASSES):
                 cols = slice((b * PASSES + g) * P, (b * PASSES + g + 1) * P)
@@ -253,135 +244,119 @@ def tile_attention_pa_kernel(tc, x_bytes, x_scale, wq, wk, out_0, out_1):
                     start=(g == 0),
                     stop=(g == PASSES - 1),
                 )
-            return acc
+            banks[j] = acc
 
-        def mm(j):
-            a, b, m = units[j]
-            even = project(a, b, 2 * m)
-            odd = project(a, b, 2 * m + 1)
-            sums[j] = (even, odd)
+        products = {}
 
-        pair = {}
-        waiting = []
+        def store(a, b, m, halves, tile_ap):
+            nc.sync.dma_start(
+                out=outs[m][b, a * P:(a + 1) * P, halves.start * 512:halves.stop * 512].rearrange(
+                    "t (h f) -> t h f", f=512),
+                in_=tile_ap)
 
-        def store(j, tile_ap, first_col, last_col):
-            a, b, m = units[j]
-            nc.sync.dma_start(out=outs[m][b, a * P:(a + 1) * P, first_col:last_col], in_=tile_ap)
+        def add_and_store(a, b, m, halves, engine_add):
+            prod = products[(a, b, m)]
+            engine_add(out=prod[:, halves, 0, :], in0=prod[:, halves, 0, :], in1=prod[:, halves, 1, :], op=ALU.add)
+            store(a, b, m, halves, prod[:, halves, 0, :])
 
-        def vector_adds():
-            for j, pt, qt, cols, base in waiting:
-                nc.vector.tensor_tensor(out=pt[:, cols], in0=pt[:, cols], in1=qt[:, cols], op=ALU.add)
-                store(j, pt[:, cols], cols.start - base, cols.stop - base)
-            waiting.clear()
+        def vg(j):
+            a, b, c = pieces[j]
+            m, h = c // 2, c % 2
+            if h == 0:
+                prod_new = slabs.tile([P, 2, 2, 512], F32, name="slab")
+                products[(a, b, m)] = prod_new
+            prod = products[(a, b, m)]
+            nc.vector.tensor_tensor(
+                out=prod[:, h, :, :].rearrange("p z (i e) -> p z i e", e=2),
+                in0=tabs[a][:, :, h * HALF:(h + 1) * HALF, :],
+                in1=banks[j][:].rearrange("p (z i) -> p z i", z=2).unsqueeze(3).to_broadcast([P, 2, HALF, 2]),
+                op=ALU.mult)
+            if j == len(pieces) - 1:
+                add_and_store(a, b, m, slice(h, h + 1), nc.vector.tensor_tensor)
+            elif a == 0 or j == len(pieces) - 2:
+                add_and_store(a, b, m, slice(h, h + 1), nc.gpsimd.tensor_tensor)
+            elif h == 1:
+                add_and_store(a, b, m, slice(0, 2), nc.gpsimd.tensor_tensor)
 
-        def by_vector(j):
-            return j % VECTOR_ADDS_EVERY == VECTOR_ADDS_EVERY - 1
-
-        def vg(j, pieces=1):
-            a, b, m = units[j]
-            even, odd = sums[j]
-            if j % 2 == 0:
-                pt_new = slabs.tile([P, 2 * E], F32, name="slab")
-                qt_new = slabs.tile([P, 2 * E], F32, name="slab")
-                pair["t"] = (pt_new, qt_new)
-            pt, qt = pair["t"]
-            base = (j % 2) * E
-            step = PAIRS // pieces
-            for h in range(pieces):
-                pr = slice(h * step, (h + 1) * step)
-                cols = slice(base + 2 * h * step, base + 2 * (h + 1) * step)
-                nc.vector.tensor_tensor(out=pt[:, cols].rearrange("p (i e) -> p i e", e=2),
-                                        in0=tabs[a][0][:, pr, :],
-                                        in1=even[:, pr].unsqueeze(2).to_broadcast([P, step, 2]), op=ALU.mult)
-                if j % 2 == 0:
-                    vector_adds()
-                nc.vector.tensor_tensor(out=qt[:, cols].rearrange("p (i e) -> p i e", e=2),
-                                        in0=tabs[a][1][:, pr, :],
-                                        in1=odd[:, pr].unsqueeze(2).to_broadcast([P, step, 2]), op=ALU.mult)
-                if by_vector(j):
-                    waiting.append((j, pt, qt, cols, base))
-            if not by_vector(j):
-                nc.gpsimd.tensor_tensor(out=pt[:, base:base + E], in0=pt[:, base:base + E], in1=qt[:, base:base + E],
-                                        op=ALU.add)
-                store(j, pt[:, base:base + E], 0, E)
-
+        s_copy, v_copy = nc.scalar.copy, nc.vector.tensor_copy
         cast_group(1, nc.gpsimd.tensor_copy)
-        cast_group(2, nc.gpsimd.tensor_copy)
-        table_turns([0])
+        table_turns(0)
         planes_on_vector(0)
+        spread_scales(0)
+        spread_scales(1)
         tables(0)
+        turn_w(0, 0, v_copy)
+        turn_w(0, 1, v_copy)
+        turn_w(0, 2, s_copy)
+        turn_w(0, 3, s_copy)
         widen(0)
-        turn_x(0)
         widen(1)
-        quant_x(0)
-        widen(2)
-        widen(3)
-        table_turns([1, 2, 3])
-        turn_w(0)
-        quant_w(0)
-        turn_w(1)
+        turn_x(0)
         turn_x(1)
-        turn_x(2)
-        quant_w(1)
+        quant_w(0)
+        quant_x(0)
         quant_x(1)
-        quant_x(2)
+        turn_w(1, 0, s_copy)
+        turn_w(1, 1, s_copy)
         mm(0)
-        turn_x(3)
-        planes_on_scalar(1)
-        tables(1)
         mm(1)
-        mm(2)
-        turn_w(2)
+        widen(2)
+        turn_w(1, 2, s_copy)
+        turn_w(1, 3, s_copy)
+        turn_x(2)
         vg(0)
+        widen(3)
+        turn_w(2, 0, s_copy)
+        turn_w(2, 1, s_copy)
+        turn_x(3)
+        vg(1)
+        quant_x(2)
+        mm(2)
+        table_turns(1)
         quant_x(3)
         mm(3)
-        turn_w(3)
-        vg(1)
+        turn_w(2, 2, s_copy)
+        turn_w(2, 3, s_copy)
+        quant_w(1)
         vg(2)
-        quant_w(2)
-        quant_w(3)
-        bank(1, 0)
-        bank(1, 1)
+        vg(3)
         mm(4)
         mm(5)
-        vg(3)
-        mm(6)
-        bank(1, 2)
+        turn_w(3, 0, s_copy)
+        turn_w(3, 1, s_copy)
+        table_turns(2)
         vg(4)
-        mm(7)
-        bank(1, 3)
-        cast_group(3, nc.scalar.copy)
-        planes_on_scalar(2)
-        tables(2)
-        planes_on_scalar(3)
-        tables(3)
+        mm(6)
+        turn_w(3, 2, s_copy)
+        turn_w(3, 3, s_copy)
+        table_turns(3)
         vg(5)
-        vg(6)
-        vg(7)
-        quant_group(1, 0)
-        mm(8)
-        mm(9)
-        mm(10)
-        quant_group(1, 1)
-        bank(2, 0)
-        bank(2, 1)
-        for j in range(8, len(units)):
-            if j in (13, 21):
-                quant_group(j // 8 + 1, 0)
-            if j in (14, 22):
-                quant_group(j // 8 + 1, 1)
-            vg(j, 2 if j == len(units) - 1 else 1)
-            if 10 < j + 3 < len(units):
-                mm(j + 3)
-            if j == 8:
-                bank(2, 2)
-            if j == 9:
-                bank(2, 3)
-            if j == 15:
-                bank(3, 0)
-                bank(3, 1)
-            if j == 16:
-                bank(3, 2)
-            if j == 17:
-                bank(3, 3)
-        vector_adds()
+        mm(7)
+        bank(1, 0)
+        quant_w(2)
+
+        def make_table(a):
+            planes_on_scalar(a)
+            tables(a)
+
+        before = {8: [(quant_w, (3,))]}
+        behind = {6: [(bank, (1, 1))], 7: [(bank, (1, 2))], 9: [(bank, (1, 3)), (make_table, (1,))]}
+        for a in range(1, POS_TILES):
+            before[16 * a - LATE] = [(quant_group, (a, 0))]
+            before[16 * a + 2] = [(quant_group, (a, 1))]
+        for a in range(2, POS_TILES):
+            first = 16 * (a - 1)
+            behind[first - 4] = [(cast_group, (a, s_copy))]
+            for k, step in enumerate((0, 1, 3, 5)):
+                behind[first + step] = [(bank, (a, k))]
+            behind[first + 6] = [(make_table, (a,))]
+        mm_next = 8
+        for j in range(6, len(pieces)):
+            for step, what in before.get(j, []):
+                step(*what)
+            vg(j)
+            while mm_next < len(pieces) and mm_next <= j + AHEAD and j >= 16 * pieces[mm_next][0] - LATE:
+                mm(mm_next)
+                mm_next += 1
+            for step, what in behind.get(j, []):
+                step(*what)

@@ -26,6 +26,7 @@ PASSES = D // 512
 TWO_PI = 2.0 * math.pi
 REDUCED = 288
 AHEAD = 4
+VECTOR_ADDS = (61, 63)
 LATE = 2
 
 
@@ -37,7 +38,7 @@ def tile_attention_pa_kernel(tc, x_bytes, x_scale, wq, wk, out_0, out_1):
     with ExitStack() as ctx:
         const = ctx.enter_context(tc.tile_pool(name="const", bufs=1))
         tabp = ctx.enter_context(tc.tile_pool(name="tabp", bufs=4))
-        argp = ctx.enter_context(tc.tile_pool(name="argp", bufs=3))
+        argp = ctx.enter_context(tc.tile_pool(name="argp", bufs=2))
         xwp = ctx.enter_context(tc.tile_pool(name="xwp", bufs=3))
         xgp = ctx.enter_context(tc.tile_pool(name="xgp", bufs=3))
         xcp = ctx.enter_context(tc.tile_pool(name="xcp", bufs=2))
@@ -88,45 +89,70 @@ def tile_attention_pa_kernel(tc, x_bytes, x_scale, wq, wk, out_0, out_1):
         nc.scalar.activation(out=first_sin[:], in_=inv[:, 0:1], func=ACT.Sin)
         n = 1
         while n < PAIRS:
-            nc.vector.tensor_scalar(out=inv[:, n:2 * n], in0=inv[:, 0:n], scalar1=THETA ** (-n / float(PAIRS)),
-                                    scalar2=None, op0=ALU.mult)
-            n *= 2
+            for q in range(1, min(4, PAIRS // n)):
+                nc.vector.tensor_scalar(out=inv[:, q * n:(q + 1) * n], in0=inv[:, 0:n],
+                                        scalar1=THETA ** (-q * n / float(PAIRS)), scalar2=None, op0=ALU.mult)
+            n *= 4
         turns = const.tile([P, POS_TILES], F32, name="turns")
         nc.vector.tensor_scalar(out=turns[:], in0=tcol[:], scalar1=1.0 / TWO_PI, scalar2=None, op0=ALU.mult)
+        back = const.tile([P, POS_TILES], F32, name="back")
+        nc.vector.tensor_scalar(out=back[:], in0=tcol[:], scalar1=-1.0 / TWO_PI, scalar2=None, op0=ALU.mult)
 
         args = {}
         tabs = {}
+        whole = {}
+
+        def whole_turns(a):
+            whole_a = const.tile([P, REDUCED], I32, name="ni%d" % a)
+            whole[a] = whole_a
+            nc.vector.tensor_scalar(out=whole[a][:], in0=inv[:, 0:REDUCED], scalar1=turns[:, a:a + 1], scalar2=None,
+                                    op0=ALU.mult)
+
+        def turns_left(a, first, last, plane, col, op):
+            if plane == 2:
+                arg_new = argp.tile([P, 3, last - first], F32, name="arg%d" % (last - first))
+                args[a, first // HALF] = arg_new
+            arg = args[a, first // HALF]
+            if first < REDUCED:
+                stop = min(last, REDUCED)
+                nc.vector.scalar_tensor_tensor(out=arg[:, plane, 0:stop - first], in0=inv[:, first:stop],
+                                               scalar=col[:, a:a + 1], in1=whole[a][:, first:stop], op0=ALU.mult,
+                                               op1=op)
+            if last > REDUCED:
+                nc.vector.tensor_scalar(out=arg[:, plane, REDUCED - first:last - first], in0=inv[:, REDUCED:last],
+                                        scalar1=col[:, a:a + 1], scalar2=None, op0=ALU.mult)
 
         def table_turns(a):
-            whole = const.tile([P, REDUCED], I32, name="ni%d" % a)
-            arg_new = argp.tile([P, 3, PAIRS], F32, name="arg")
-            args[a] = arg_new
-            nc.vector.tensor_scalar(out=whole[:], in0=inv[:, 0:REDUCED], scalar1=turns[:, a:a + 1], scalar2=None,
-                                    op0=ALU.mult)
-            nc.vector.tensor_scalar(out=args[a][:, 2, REDUCED:PAIRS], in0=inv[:, REDUCED:PAIRS],
-                                    scalar1=turns[:, a:a + 1], scalar2=None, op0=ALU.mult)
-            nc.vector.scalar_tensor_tensor(out=args[a][:, 2, 0:REDUCED], in0=inv[:, 0:REDUCED],
-                                           scalar=turns[:, a:a + 1], in1=whole[:], op0=ALU.mult, op1=ALU.subtract)
+            whole_turns(a)
+            turns_left(a, 0, PAIRS, 2, turns, ALU.subtract)
 
-        def planes_on_vector(a):
-            nc.vector.tensor_scalar(out=args[a][:, 0, :], in0=args[a][:, 2, :], scalar1=-1.0, scalar2=None,
-                                    op0=ALU.mult)
-            nc.vector.tensor_tensor(out=args[a][:, 1, :], in0=args[a][:, 2, :], in1=args[a][:, 0, :], op=ALU.min)
-            nc.vector.tensor_scalar(out=args[a][:, 1, :], in0=args[a][:, 1, :], scalar1=0.25, scalar2=None,
-                                    op0=ALU.add)
+        def half_table_turns(a, h):
+            turns_left(a, h * HALF, (h + 1) * HALF, 2, turns, ALU.subtract)
+            turns_left(a, h * HALF, (h + 1) * HALF, 0, back, ALU.add)
+
+        def quarter_min(a, h):
+            arg = args[a, h]
+            nc.vector.tensor_tensor(out=arg[:, 1, :], in0=arg[:, 2, :], in1=arg[:, 0, :], op=ALU.min)
+
+        def quarter_add(a, h):
+            arg = args[a, h]
+            nc.vector.tensor_scalar(out=arg[:, 1, :], in0=arg[:, 1, :], scalar1=0.25, scalar2=None, op0=ALU.add)
 
         def planes_on_scalar(a):
-            nc.scalar.activation(out=args[a][:, 0, :], in_=args[a][:, 2, :], func=ACT.Copy, scale=-1.0)
-            nc.scalar.activation(out=args[a][:, 1, :], in_=args[a][:, 2, :], func=ACT.Abs)
-            nc.scalar.activation(out=args[a][:, 1, :], in_=args[a][:, 1, :], func=ACT.Identity, scale=-1.0, bias=0.25)
+            arg = args[a, 0]
+            nc.scalar.activation(out=arg[:, 0, :], in_=arg[:, 2, :], func=ACT.Copy, scale=-1.0)
+            nc.scalar.activation(out=arg[:, 1, :], in_=arg[:, 2, :], func=ACT.Abs)
+            nc.scalar.activation(out=arg[:, 1, :], in_=arg[:, 1, :], func=ACT.Identity, scale=-1.0, bias=0.25)
 
-        def tables(a):
-            tab = tabp.tile([P, 2, PAIRS, 2], F32, name="tab")
-            nc.scalar.activation(out=tab[:, 0, :, :], in_=args[a][:, 1:3, :].rearrange("p e i -> p i e"), func=ACT.Sin,
-                                 scale=TWO_PI)
-            nc.scalar.activation(out=tab[:, 1, :, :], in_=args[a][:, 0:2, :].rearrange("p e i -> p i e"), func=ACT.Sin,
-                                 scale=TWO_PI)
-            tabs[a] = tab
+        def tables(a, halves):
+            if halves.start == 0:
+                tab = tabp.tile([P, 2, 2, HALF, 2], F32, name="tab")
+                tabs[a] = tab
+            for z in range(2):
+                planes_read = args[a, halves.start][:, 1 - z:3 - z, :]
+                nc.scalar.activation(out=tabs[a][:, halves, z, :, :],
+                                     in_=planes_read.rearrange("p e (h i) -> p h i e", i=HALF), func=ACT.Sin,
+                                     scale=TWO_PI)
 
         xs_bc = const.tile([P, D], F32, name="xs_bc")
 
@@ -134,7 +160,7 @@ def tile_attention_pa_kernel(tc, x_bytes, x_scale, wq, wk, out_0, out_1):
             tp = tps.tile([P, 4, P], F32, name="tp")
             for t in range(4):
                 nc.tensor.transpose(tp[:, t, :], xs_col[:, g, t:t + 1].to_broadcast([P, P]), ident[:])
-            nc.vector.tensor_copy(out=xs_bc[:, 512 * g:512 * (g + 1)].rearrange("p (n t) -> p n t", t=4),
+            nc.scalar.copy(out=xs_bc[:, 512 * g:512 * (g + 1)].rearrange("p (n t) -> p n t", t=4),
                                   in_=tp[:].rearrange("p t n -> p n t"))
 
         def transpose_words(src):
@@ -213,18 +239,25 @@ def tile_attention_pa_kernel(tc, x_bytes, x_scale, wq, wk, out_0, out_1):
             if r == 0:
                 wg_new = wgp.tile([P, PASSES * 512 * 4], BF16, name="wg", align_bytes=64)
                 wgrouped[c] = wg_new
-            z, v = r // 2, r % 2
-            tp = transpose_words(wraw[c][:, v, z, :])
-            engine_copy(out=wgrouped[c][:].bitcast(F32).rearrange("p (g r u) -> p g r u", g=PASSES, u=2)
-                        [:, :, r * P:(r + 1) * P, :],
-                        in_=tp[:].rearrange("p (g u) r -> p g r u", g=PASSES))
+            g, z = r // 2, r % 2
+            tp = tps.tile([P, 4, P], F32, name="tp")
+            for v in range(2):
+                words = wraw[c][:, v, z, :].bitcast(F32)
+                for u in range(2):
+                    nc.tensor.transpose(tp[:, 2 * v + u, :], words[:, 256 * g + u:256 * (g + 1):2], ident[:])
+            stretch = slice((2 * g + z) * 512, (2 * g + z + 1) * 512)
+            engine_copy(out=wgrouped[c][:].bitcast(F32)[:, stretch].rearrange("p (v r u) -> p v r u", v=2, u=2),
+                        in_=tp[:].rearrange("p (v u) r -> p v r u", v=2))
 
-        def quant_w(c):
-            wc = const.tile([P, PASSES * 512], U32, name="wc%d" % c, align_bytes=64)
-            ws = const.tile([P, PASSES * 512], U8, name="ws%d" % c, align_bytes=64)
-            nc.vector.quantize_mx(out=wc[:].bitcast(FP8X4), scales=ws[:], in_=wgrouped[c][:])
-            wcodes[c] = wc
-            wscales[c] = ws
+        def quant_w(c, passes):
+            if passes.start == 0:
+                wc = const.tile([P, PASSES * 512], U32, name="wc%d" % c, align_bytes=64)
+                ws = const.tile([P, PASSES * 512], U8, name="ws%d" % c, align_bytes=64)
+                wcodes[c] = wc
+                wscales[c] = ws
+            cols = slice(passes.start * 512, passes.stop * 512)
+            nc.vector.quantize_mx(out=wcodes[c][:, cols].bitcast(FP8X4), scales=wscales[c][:, cols],
+                                  in_=wgrouped[c][:, 4 * cols.start:4 * cols.stop])
 
         pieces = [(0, b, c) for c in range(4) for b in range(B)]
         pieces += [(a, b, c) for a in range(1, POS_TILES) for b in range(B) for c in range(4)]
@@ -247,6 +280,7 @@ def tile_attention_pa_kernel(tc, x_bytes, x_scale, wq, wk, out_0, out_1):
             banks[j] = acc
 
         products = {}
+        parts = []
 
         def store(a, b, m, halves, tile_ap):
             nc.sync.dma_start(
@@ -268,79 +302,94 @@ def tile_attention_pa_kernel(tc, x_bytes, x_scale, wq, wk, out_0, out_1):
             prod = products[(a, b, m)]
             nc.vector.tensor_tensor(
                 out=prod[:, h, :, :].rearrange("p z (i e) -> p z i e", e=2),
-                in0=tabs[a][:, :, h * HALF:(h + 1) * HALF, :],
+                in0=tabs[a][:, h, :, :, :],
                 in1=banks[j][:].rearrange("p (z i) -> p z i", z=2).unsqueeze(3).to_broadcast([P, 2, HALF, 2]),
                 op=ALU.mult)
-            if j == len(pieces) - 1:
-                add_and_store(a, b, m, slice(h, h + 1), nc.vector.tensor_tensor)
-            elif a == 0 or j == len(pieces) - 2:
-                add_and_store(a, b, m, slice(h, h + 1), nc.gpsimd.tensor_tensor)
+            if a == 0 or j >= len(pieces) - 2:
+                parts.append((a, b, m, slice(h, h + 1), j))
             elif h == 1:
-                add_and_store(a, b, m, slice(0, 2), nc.gpsimd.tensor_tensor)
+                parts.append((a, b, m, slice(0, 2), j))
+            while parts and (parts[0][4] not in VECTOR_ADDS or parts[0][4] < j or j == len(pieces) - 1):
+                pa, pb, pm, halves, pj = parts.pop(0)
+                add_and_store(pa, pb, pm, halves,
+                              nc.vector.tensor_tensor if pj in VECTOR_ADDS else nc.gpsimd.tensor_tensor)
 
         s_copy, v_copy = nc.scalar.copy, nc.vector.tensor_copy
-        cast_group(1, nc.gpsimd.tensor_copy)
-        table_turns(0)
-        planes_on_vector(0)
-        spread_scales(0)
-        spread_scales(1)
-        tables(0)
-        turn_w(0, 0, v_copy)
-        turn_w(0, 1, v_copy)
-        turn_w(0, 2, s_copy)
-        turn_w(0, 3, s_copy)
-        widen(0)
-        widen(1)
-        turn_x(0)
-        turn_x(1)
-        quant_w(0)
-        quant_x(0)
-        quant_x(1)
-        turn_w(1, 0, s_copy)
-        turn_w(1, 1, s_copy)
-        mm(0)
-        mm(1)
-        widen(2)
-        turn_w(1, 2, s_copy)
-        turn_w(1, 3, s_copy)
-        turn_x(2)
-        vg(0)
-        widen(3)
-        turn_w(2, 0, s_copy)
-        turn_w(2, 1, s_copy)
-        turn_x(3)
-        vg(1)
-        quant_x(2)
-        mm(2)
-        table_turns(1)
-        quant_x(3)
-        mm(3)
-        turn_w(2, 2, s_copy)
-        turn_w(2, 3, s_copy)
-        quant_w(1)
-        vg(2)
-        vg(3)
-        mm(4)
-        mm(5)
-        turn_w(3, 0, s_copy)
-        turn_w(3, 1, s_copy)
-        table_turns(2)
-        vg(4)
-        mm(6)
-        turn_w(3, 2, s_copy)
-        turn_w(3, 3, s_copy)
-        table_turns(3)
-        vg(5)
-        mm(7)
-        bank(1, 0)
-        quant_w(2)
 
         def make_table(a):
             planes_on_scalar(a)
-            tables(a)
+            tables(a, slice(0, 2))
 
-        before = {8: [(quant_w, (3,))]}
-        behind = {6: [(bank, (1, 1))], 7: [(bank, (1, 2))], 9: [(bank, (1, 3)), (make_table, (1,))]}
+        cast_group(1, nc.gpsimd.tensor_copy)
+        whole_turns(0)
+        half_table_turns(0, 0)
+        whole_turns(1)
+        quarter_min(0, 0)
+        whole_turns(2)
+        quarter_add(0, 0)
+        whole_turns(3)
+        turns_left(1, 0, PAIRS, 2, turns, ALU.subtract)
+        spread_scales(0)
+        spread_scales(1)
+        turn_w(0, 0, v_copy)
+        turn_w(0, 1, s_copy)
+        turn_w(0, 2, s_copy)
+        turn_w(0, 3, s_copy)
+        tables(0, slice(0, 1))
+        widen(0)
+        turn_x(0)
+        half_table_turns(0, 1)
+        quant_w(0, slice(0, 1))
+        quarter_min(0, 1)
+        quant_w(0, slice(1, 2))
+        quarter_add(0, 1)
+        turn_w(1, 0, s_copy)
+        turn_w(1, 1, s_copy)
+        turn_w(1, 2, s_copy)
+        turn_w(1, 3, s_copy)
+        widen(1)
+        quant_x(0)
+        mm(0)
+        turn_x(1)
+        widen(2)
+        turn_x(2)
+        turn_w(2, 0, s_copy)
+        turn_w(2, 1, s_copy)
+        vg(0)
+        widen(3)
+        turn_w(2, 2, s_copy)
+        turn_w(2, 3, s_copy)
+        quant_x(1)
+        mm(1)
+        quant_x(2)
+        turn_x(3)
+        mm(2)
+        tables(0, slice(1, 2))
+        turn_w(3, 0, s_copy)
+        turn_w(3, 1, s_copy)
+        vg(1)
+        quant_x(3)
+        turn_w(3, 2, s_copy)
+        turn_w(3, 3, s_copy)
+        vg(2)
+        mm(3)
+        quant_w(1, slice(0, 2))
+        bank(1, 0)
+        mm(4)
+        vg(3)
+        turns_left(2, 0, PAIRS, 2, turns, ALU.subtract)
+        bank(1, 1)
+        mm(5)
+        vg(4)
+        mm(6)
+        quant_w(2, slice(0, 2))
+        bank(1, 2)
+        vg(5)
+        mm(7)
+        make_table(1)
+
+        before = {8: [(quant_w, (3, slice(0, 2)))], 11: [(turns_left, (3, 0, PAIRS, 2, turns, ALU.subtract))]}
+        behind = {6: [(bank, (1, 3))]}
         for a in range(1, POS_TILES):
             before[16 * a - LATE] = [(quant_group, (a, 0))]
             before[16 * a + 2] = [(quant_group, (a, 1))]

@@ -224,12 +224,12 @@ def tile_attention_pa_kernel(tc, x_bytes, x_scale, wq, wk, out_0, out_1):
                 if g == 0:
                     xg4_new = xg4p.tile([P, B * PASSES * P * 4], BF16, name="xg4", align_bytes=64)
                     grouped4[a] = xg4_new
-                xg4v = grouped4[a][:].rearrange("p (b g r t) -> p b g r t", b=B, g=PASSES, t=4)
-                nc.scalar.copy(out=xg4v[:, :, g, :, :],
-                               in_=planes[a][:, g, :, :].rearrange("p t (b r) -> p b r t", b=B))
+                width = B * P * 4
+                nc.scalar.copy(out=grouped4[a][:, g * width:(g + 1) * width].rearrange("p (c i t) -> p c t i", i=4, t=4),
+                               in_=planes[a][:, g, :, :].rearrange("p t (c i) -> p c t i", i=4))
 
-        def quant_group(a, half):
-            cols = slice(half * 2 * PASSES * P, (half + 1) * 2 * PASSES * P)
+        def quant_group(a, g):
+            cols = slice(g * B * P, (g + 1) * B * P)
             nc.vector.quantize_mx(out=xcodes[a][:, cols].bitcast(FP8X4), scales=xscales[a][:, cols],
                                   in_=grouped4[a][:, 4 * cols.start:4 * cols.stop])
 
@@ -267,7 +267,8 @@ def tile_attention_pa_kernel(tc, x_bytes, x_scale, wq, wk, out_0, out_1):
             a, b, c = pieces[j]
             acc = accp.tile([P, 512], F32, name="acc")
             for g in range(PASSES):
-                cols = slice((b * PASSES + g) * P, (b * PASSES + g + 1) * P)
+                first = (b * PASSES + g) * P if a == 0 else (g * B + b) * P
+                cols = slice(first, first + P)
                 nc.tensor.matmul_mx(
                     out=acc[:],
                     lhsT=xcodes[a][:, cols].bitcast(FP8X4),
@@ -356,43 +357,42 @@ def tile_attention_pa_kernel(tc, x_bytes, x_scale, wq, wk, out_0, out_1):
         turn_w(2, 0, s_copy)
         turn_w(2, 1, s_copy)
         vg(0)
+        quant_x(1)
+        mm(1)
         widen(3)
         turn_w(2, 2, s_copy)
         turn_w(2, 3, s_copy)
-        quant_x(1)
-        mm(1)
-        quant_x(2)
         turn_x(3)
+        vg(1)
+        quant_x(2)
         mm(2)
+        quant_w(1, slice(0, 2))
         tables(0, slice(1, 2))
         turn_w(3, 0, s_copy)
         turn_w(3, 1, s_copy)
-        vg(1)
         quant_x(3)
+        mm(3)
+        vg(2)
         turn_w(3, 2, s_copy)
         turn_w(3, 3, s_copy)
-        vg(2)
-        mm(3)
-        quant_w(1, slice(0, 2))
-        bank(1, 0)
         mm(4)
         vg(3)
-        turns_left(2, 0, PAIRS, 2, turns, ALU.subtract)
-        bank(1, 1)
+        bank(1, 0)
         mm(5)
         vg(4)
         mm(6)
+        bank(1, 1)
+        turns_left(2, 0, PAIRS, 2, turns, ALU.subtract)
         quant_w(2, slice(0, 2))
-        bank(1, 2)
         vg(5)
         mm(7)
+        bank(1, 2)
         make_table(1)
 
-        before = {8: [(quant_w, (3, slice(0, 2)))], 11: [(turns_left, (3, 0, PAIRS, 2, turns, ALU.subtract))]}
+        before = {8: [(quant_w, (3, slice(0, 2)))], 13: [(turns_left, (3, 0, PAIRS, 2, turns, ALU.subtract))]}
         behind = {6: [(bank, (1, 3))]}
         for a in range(1, POS_TILES):
-            before[16 * a - LATE] = [(quant_group, (a, 0))]
-            before[16 * a + 2] = [(quant_group, (a, 1))]
+            before[16 * a - LATE] = [(quant_group, (a, 0)), (quant_group, (a, 1))]
         for a in range(2, POS_TILES):
             first = 16 * (a - 1)
             behind[first - 4] = [(cast_group, (a, s_copy))]

@@ -27,6 +27,7 @@ TWO_PI = 2.0 * math.pi
 REDUCED = 288
 AHEAD = 4
 VECTOR_ADDS = (61, 63)
+TENSOR_ADDS = (29, 43, 51, 57)
 LATE = 2
 
 
@@ -282,6 +283,7 @@ def tile_attention_pa_kernel(tc, x_bytes, x_scale, wq, wk, out_0, out_1):
 
         products = {}
         parts = []
+        waiting = []
 
         def store(a, b, m, halves, tile_ap):
             nc.sync.dma_start(
@@ -293,6 +295,19 @@ def tile_attention_pa_kernel(tc, x_bytes, x_scale, wq, wk, out_0, out_1):
             prod = products[(a, b, m)]
             engine_add(out=prod[:, halves, 0, :], in0=prod[:, halves, 0, :], in1=prod[:, halves, 1, :], op=ALU.add)
             store(a, b, m, halves, prod[:, halves, 0, :])
+
+        def add_on_tensor(a, b, m, halves):
+            prod = products[(a, b, m)]
+            tp = tps.tile([P, 4, P], F32, name="tp")
+            total = tp[:].rearrange("p v r -> p (v r)")
+            for z in range(2):
+                nc.tensor.matmul(total, lhsT=ident[:], rhs=prod[:, halves.start, z, :], start=(z == 0), stop=(z == 1))
+            nc.scalar.copy(out=prod[:, halves.start, 0, :], in_=total)
+            store(a, b, m, halves, prod[:, halves, 0, :])
+
+        def tensor_sums(j):
+            while waiting and waiting[0][0] <= j - 2:
+                add_on_tensor(*waiting.pop(0)[1])
 
         def vg(j):
             a, b, c = pieces[j]
@@ -306,14 +321,17 @@ def tile_attention_pa_kernel(tc, x_bytes, x_scale, wq, wk, out_0, out_1):
                 in0=tabs[a][:, h, :, :, :],
                 in1=banks[j][:].rearrange("p (z i) -> p z i", z=2).unsqueeze(3).to_broadcast([P, 2, HALF, 2]),
                 op=ALU.mult)
-            if a == 0 or j >= len(pieces) - 2:
-                parts.append((a, b, m, slice(h, h + 1), j))
+            on_tensor = (j | 1) in TENSOR_ADDS
+            if on_tensor:
+                waiting.append((j, (a, b, m, slice(h, h + 1))))
+            elif a == 0 or j >= len(pieces) - 2:
+                parts.append((j, (a, b, m, slice(h, h + 1))))
             elif h == 1:
-                parts.append((a, b, m, slice(0, 2), j))
-            while parts and (parts[0][4] not in VECTOR_ADDS or parts[0][4] < j or j == len(pieces) - 1):
-                pa, pb, pm, halves, pj = parts.pop(0)
-                add_and_store(pa, pb, pm, halves,
-                              nc.vector.tensor_tensor if pj in VECTOR_ADDS else nc.gpsimd.tensor_tensor)
+                parts.append((j, (a, b, m, slice(0, 2))))
+            while parts and (parts[0][0] not in VECTOR_ADDS or parts[0][0] < j or j == len(pieces) - 1):
+                done, what = parts.pop(0)
+                add_and_store(*what, nc.vector.tensor_tensor if done in VECTOR_ADDS else nc.gpsimd.tensor_tensor)
+
 
         s_copy, v_copy = nc.scalar.copy, nc.vector.tensor_copy
 
@@ -407,5 +425,6 @@ def tile_attention_pa_kernel(tc, x_bytes, x_scale, wq, wk, out_0, out_1):
             while mm_next < len(pieces) and mm_next <= j + AHEAD and j >= 16 * pieces[mm_next][0] - LATE:
                 mm(mm_next)
                 mm_next += 1
+            tensor_sums(j)
             for step, what in behind.get(j, []):
                 step(*what)

@@ -79,6 +79,13 @@ def tile_attention_pa_kernel(tc, x_bytes, x_scale, wq, wk, out_0, out_1):
         load_x(2)
         load_x(3)
 
+        zeros = const.tile([P, 512], BF16, name="zeros")
+        nc.gpsimd.memset(zeros[:], 0.0)
+
+        def keep_clock():
+            acc = accp.tile([P, 512], F32, name="acc")
+            nc.tensor.matmul(acc[:], lhsT=zeros[:, 0:P], rhs=zeros[:], start=True, stop=True)
+
         tcol = const.tile([P, POS_TILES], F32, name="tcol")
         nc.gpsimd.iota(tcol[:], pattern=[[P, POS_TILES]], base=0, channel_multiplier=1,
                        allow_small_or_imprecise_dtypes=True)
@@ -348,15 +355,25 @@ def tile_attention_pa_kernel(tc, x_bytes, x_scale, wq, wk, out_0, out_1):
         quarter_add(0, 0)
         whole_turns(3)
         turns_left(1, 0, PAIRS, 2, turns, ALU.subtract)
+        keep_clock()
+        keep_clock()
+        keep_clock()
+        keep_clock()
         spread_scales(0)
         spread_scales(1)
+        keep_clock()
+        keep_clock()
         turn_w(0, 0, v_copy)
         turn_w(0, 1, s_copy)
+        keep_clock()
         turn_w(0, 2, s_copy)
         turn_w(0, 3, s_copy)
+        keep_clock()
         tables(0, slice(0, 1))
         widen(0)
         turn_x(0)
+        keep_clock()
+        keep_clock()
         half_table_turns(0, 1)
         quant_w(0, slice(0, 1))
         quarter_min(0, 1)
@@ -364,8 +381,10 @@ def tile_attention_pa_kernel(tc, x_bytes, x_scale, wq, wk, out_0, out_1):
         quarter_add(0, 1)
         turn_w(1, 0, s_copy)
         turn_w(1, 1, s_copy)
+        keep_clock()
         turn_w(1, 2, s_copy)
         turn_w(1, 3, s_copy)
+        keep_clock()
         widen(1)
         quant_x(0)
         mm(0)
@@ -374,6 +393,7 @@ def tile_attention_pa_kernel(tc, x_bytes, x_scale, wq, wk, out_0, out_1):
         turn_x(2)
         turn_w(2, 0, s_copy)
         turn_w(2, 1, s_copy)
+        keep_clock()
         vg(0)
         quant_x(1)
         mm(1)
@@ -388,6 +408,7 @@ def tile_attention_pa_kernel(tc, x_bytes, x_scale, wq, wk, out_0, out_1):
         tables(0, slice(1, 2))
         turn_w(3, 0, s_copy)
         turn_w(3, 1, s_copy)
+        keep_clock()
         quant_x(3)
         mm(3)
         vg(2)

@@ -26,8 +26,7 @@ PASSES = D // 512
 TWO_PI = 2.0 * math.pi
 REDUCED = 288
 AHEAD = 4
-VECTOR_ADDS = (61, 63)
-TENSOR_ADDS = (29, 43, 51, 57)
+TENSOR_ADDS = (27, 35, 43, 51, 59)
 LATE = 2
 
 
@@ -289,55 +288,57 @@ def tile_attention_pa_kernel(tc, x_bytes, x_scale, wq, wk, out_0, out_1):
             banks[j] = acc
 
         products = {}
-        parts = []
         waiting = []
 
-        def store(a, b, m, halves, tile_ap):
-            nc.sync.dma_start(
-                out=outs[m][b, a * P:(a + 1) * P, halves.start * 512:halves.stop * 512].rearrange(
-                    "t (h f) -> t h f", f=512),
-                in_=tile_ap)
+        def store(a, b, m, first, tile_ap):
+            nc.sync.dma_start(out=outs[m][b, a * P:(a + 1) * P, first:first + tile_ap.shape[1]], in_=tile_ap)
 
-        def add_and_store(a, b, m, halves, engine_add):
-            prod = products[(a, b, m)]
-            engine_add(out=prod[:, halves, 0, :], in0=prod[:, halves, 0, :], in1=prod[:, halves, 1, :], op=ALU.add)
-            store(a, b, m, halves, prod[:, halves, 0, :])
-
-        def add_on_tensor(a, b, m, halves):
-            prod = products[(a, b, m)]
+        def add_on_tensor(a, b, m, h, prod):
             tp = tps.tile([P, 4, P], F32, name="tp")
             total = tp[:].rearrange("p v r -> p (v r)")
             for z in range(2):
-                nc.tensor.matmul(total, lhsT=ident[:], rhs=prod[:, halves.start, z, :], start=(z == 0), stop=(z == 1))
-            nc.scalar.copy(out=prod[:, halves.start, 0, :], in_=total)
-            store(a, b, m, halves, prod[:, halves, 0, :])
+                nc.tensor.matmul(total, lhsT=ident[:], rhs=prod[:, z, :], start=(z == 0), stop=(z == 1))
+            nc.scalar.copy(out=prod[:, 0, :], in_=total)
+            store(a, b, m, h * 512, prod[:, 0, :])
 
         def tensor_sums(j):
             while waiting and waiting[0][0] <= j - 2:
                 add_on_tensor(*waiting.pop(0)[1])
 
+        def multiply(a, h, first, last, out, bank_cols):
+            nc.vector.tensor_tensor(
+                out=out.rearrange("p z (i e) -> p z i e", e=2),
+                in0=tabs[a][:, h, :, first:last, :],
+                in1=bank_cols[:, :, first:last].unsqueeze(3).to_broadcast([P, 2, last - first, 2]),
+                op=ALU.mult)
+
+        def add(prod, engine_add):
+            engine_add(out=prod[:, 0, :], in0=prod[:, 0, :], in1=prod[:, 1, :], op=ALU.add)
+
         def vg(j):
             a, b, c = pieces[j]
             m, h = c // 2, c % 2
+            bank_cols = banks[j][:].rearrange("p (z i) -> p z i", z=2)
+            if j == len(pieces) - 1:
+                ends = []
+                for s in range(2):
+                    end = slabs.tile([P, 2, HALF], F32, name="slab")
+                    multiply(a, h, s * P, (s + 1) * P, end[:], bank_cols)
+                    ends.append(end)
+                for s in range(2):
+                    add(ends[s][:], nc.vector.tensor_tensor)
+                    store(a, b, m, h * 512 + s * HALF, ends[s][:, 0, :])
+                return
             if h == 0:
                 prod_new = slabs.tile([P, 2, 2, 512], F32, name="slab")
                 products[(a, b, m)] = prod_new
-            prod = products[(a, b, m)]
-            nc.vector.tensor_tensor(
-                out=prod[:, h, :, :].rearrange("p z (i e) -> p z i e", e=2),
-                in0=tabs[a][:, h, :, :, :],
-                in1=banks[j][:].rearrange("p (z i) -> p z i", z=2).unsqueeze(3).to_broadcast([P, 2, HALF, 2]),
-                op=ALU.mult)
-            on_tensor = (j | 1) in TENSOR_ADDS
-            if on_tensor:
-                waiting.append((j, (a, b, m, slice(h, h + 1))))
-            elif a == 0 or j >= len(pieces) - 2:
-                parts.append((j, (a, b, m, slice(h, h + 1))))
-            elif h == 1:
-                parts.append((j, (a, b, m, slice(0, 2))))
-            while parts and (parts[0][0] not in VECTOR_ADDS or parts[0][0] < j or j == len(pieces) - 1):
-                done, what = parts.pop(0)
-                add_and_store(*what, nc.vector.tensor_tensor if done in VECTOR_ADDS else nc.gpsimd.tensor_tensor)
+            prod = products[(a, b, m)][:, h, :, :]
+            multiply(a, h, 0, HALF, prod, bank_cols)
+            if (j | 1) in TENSOR_ADDS:
+                waiting.append((j, (a, b, m, h, prod)))
+            else:
+                add(prod, nc.gpsimd.tensor_tensor)
+                store(a, b, m, h * 512, prod[:, 0, :])
 
 
         s_copy, v_copy = nc.scalar.copy, nc.vector.tensor_copy

@@ -26,7 +26,8 @@ PASSES = D // 512
 TWO_PI = 2.0 * math.pi
 REDUCED = 288
 AHEAD = 4
-TENSOR_ADDS = (27, 35, 43, 51, 59)
+TENSOR_FROM = 20
+TENSOR_EVERY = 5
 LATE = 2
 
 
@@ -94,16 +95,18 @@ def tile_attention_pa_kernel(tc, x_bytes, x_scale, wq, wk, out_0, out_1):
         nc.vector.memset(inv[:, 0:1], 1.0)
         first_sin = const.tile([P, 1], F32, name="first_sin")
         nc.scalar.activation(out=first_sin[:], in_=inv[:, 0:1], func=ACT.Sin)
+        turns = const.tile([P, POS_TILES], F32, name="turns")
+        back = const.tile([P, POS_TILES], F32, name="back")
         n = 1
         while n < PAIRS:
             for q in range(1, min(4, PAIRS // n)):
                 nc.vector.tensor_scalar(out=inv[:, q * n:(q + 1) * n], in0=inv[:, 0:n],
                                         scalar1=THETA ** (-q * n / float(PAIRS)), scalar2=None, op0=ALU.mult)
             n *= 4
-        turns = const.tile([P, POS_TILES], F32, name="turns")
-        nc.vector.tensor_scalar(out=turns[:], in0=tcol[:], scalar1=1.0 / TWO_PI, scalar2=None, op0=ALU.mult)
-        back = const.tile([P, POS_TILES], F32, name="back")
-        nc.vector.tensor_scalar(out=back[:], in0=tcol[:], scalar1=-1.0 / TWO_PI, scalar2=None, op0=ALU.mult)
+            if n == 4:
+                nc.vector.tensor_scalar(out=turns[:], in0=tcol[:], scalar1=1.0 / TWO_PI, scalar2=None, op0=ALU.mult)
+            if n == 16:
+                nc.vector.tensor_scalar(out=back[:], in0=tcol[:], scalar1=-1.0 / TWO_PI, scalar2=None, op0=ALU.mult)
 
         args = {}
         tabs = {}
@@ -145,8 +148,8 @@ def tile_attention_pa_kernel(tc, x_bytes, x_scale, wq, wk, out_0, out_1):
             arg = args[a, h]
             nc.vector.tensor_scalar(out=arg[:, 1, :], in0=arg[:, 1, :], scalar1=0.25, scalar2=None, op0=ALU.add)
 
-        def planes_on_scalar(a):
-            arg = args[a, 0]
+        def planes_on_scalar(a, h=0):
+            arg = args[a, h]
             nc.scalar.activation(out=arg[:, 0, :], in_=arg[:, 2, :], func=ACT.Copy, scale=-1.0)
             nc.scalar.activation(out=arg[:, 1, :], in_=arg[:, 2, :], func=ACT.Abs)
             nc.scalar.activation(out=arg[:, 1, :], in_=arg[:, 1, :], func=ACT.Identity, scale=-1.0, bias=0.25)
@@ -289,6 +292,13 @@ def tile_attention_pa_kernel(tc, x_bytes, x_scale, wq, wk, out_0, out_1):
 
         products = {}
         waiting = []
+        behind_one = []
+
+        def by_vector(j):
+            return j == len(pieces) - 2
+
+        def by_tensor(j):
+            return j % TENSOR_EVERY == 2 and TENSOR_FROM <= j < len(pieces) - 2
 
         def store(a, b, m, first, tile_ap):
             nc.sync.dma_start(out=outs[m][b, a * P:(a + 1) * P, first:first + tile_ap.shape[1]], in_=tile_ap)
@@ -315,6 +325,12 @@ def tile_attention_pa_kernel(tc, x_bytes, x_scale, wq, wk, out_0, out_1):
         def add(prod, engine_add):
             engine_add(out=prod[:, 0, :], in0=prod[:, 0, :], in1=prod[:, 1, :], op=ALU.add)
 
+        def vector_sums():
+            for a, b, m, h, prod in behind_one:
+                add(prod, nc.vector.tensor_tensor)
+                store(a, b, m, h * 512, prod[:, 0, :])
+            behind_one.clear()
+
         def vg(j):
             a, b, c = pieces[j]
             m, h = c // 2, c % 2
@@ -325,6 +341,7 @@ def tile_attention_pa_kernel(tc, x_bytes, x_scale, wq, wk, out_0, out_1):
                     end = slabs.tile([P, 2, HALF], F32, name="slab")
                     multiply(a, h, s * P, (s + 1) * P, end[:], bank_cols)
                     ends.append(end)
+                vector_sums()
                 for s in range(2):
                     add(ends[s][:], nc.vector.tensor_tensor)
                     store(a, b, m, h * 512 + s * HALF, ends[s][:, 0, :])
@@ -334,8 +351,11 @@ def tile_attention_pa_kernel(tc, x_bytes, x_scale, wq, wk, out_0, out_1):
                 products[(a, b, m)] = prod_new
             prod = products[(a, b, m)][:, h, :, :]
             multiply(a, h, 0, HALF, prod, bank_cols)
-            if (j | 1) in TENSOR_ADDS:
+            vector_sums()
+            if by_tensor(j):
                 waiting.append((j, (a, b, m, h, prod)))
+            elif by_vector(j):
+                behind_one.append((a, b, m, h, prod))
             else:
                 add(prod, nc.gpsimd.tensor_tensor)
                 store(a, b, m, h * 512, prod[:, 0, :])
@@ -364,7 +384,7 @@ def tile_attention_pa_kernel(tc, x_bytes, x_scale, wq, wk, out_0, out_1):
         spread_scales(1)
         keep_clock()
         keep_clock()
-        turn_w(0, 0, v_copy)
+        turn_w(0, 0, s_copy)
         turn_w(0, 1, s_copy)
         keep_clock()
         turn_w(0, 2, s_copy)
@@ -394,7 +414,6 @@ def tile_attention_pa_kernel(tc, x_bytes, x_scale, wq, wk, out_0, out_1):
         turn_x(2)
         turn_w(2, 0, s_copy)
         turn_w(2, 1, s_copy)
-        keep_clock()
         vg(0)
         quant_x(1)
         mm(1)
@@ -409,7 +428,6 @@ def tile_attention_pa_kernel(tc, x_bytes, x_scale, wq, wk, out_0, out_1):
         tables(0, slice(1, 2))
         turn_w(3, 0, s_copy)
         turn_w(3, 1, s_copy)
-        keep_clock()
         quant_x(3)
         mm(3)
         vg(2)

from contextlib import ExitStack
import math

import concourse.mybir as mybir
from concourse.masks import make_identity

B, S, D, E = 4, 512, 1024, 1024
THETA = 10000.0
FLOPS = 2 * B * S * D * 2 * E

F32 = mybir.dt.float32
BF16 = mybir.dt.bfloat16
I32 = mybir.dt.int32
U32 = mybir.dt.uint32
U8 = mybir.dt.uint8
FP8 = mybir.dt.float8_e4m3fn
FP8X4 = mybir.dt.float8_e4m3fn_x4
ALU = mybir.AluOpType
ACT = mybir.ActivationFunctionType

P = 128
PAIRS = E // 2
HALF = PAIRS // 2
POS_TILES = S // P
PASSES = D // 512
TWO_PI = 2.0 * math.pi
REDUCED = 288
AHEAD = 4
TENSOR_FROM = 20
TENSOR_EVERY = 5
LATE = 2


def tile_attention_pa_kernel(tc, x_bytes, x_scale, wq, wk, out_0, out_1):
    nc = tc.nc
    outs = (out_0, out_1)
    weights = (wq, wk)

    with ExitStack() as ctx:
        const = ctx.enter_context(tc.tile_pool(name="const", bufs=1))
        tabp = ctx.enter_context(tc.tile_pool(name="tabp", bufs=4))
        argp = ctx.enter_context(tc.tile_pool(name="argp", bufs=2))
        xwp = ctx.enter_context(tc.tile_pool(name="xwp", bufs=3))
        xgp = ctx.enter_context(tc.tile_pool(name="xgp", bufs=3))
        xcp = ctx.enter_context(tc.tile_pool(name="xcp", bufs=2))
        xg4p = ctx.enter_context(tc.tile_pool(name="xg4p", bufs=1))
        xplp = ctx.enter_context(tc.tile_pool(name="xplp", bufs=1))
        wgp = ctx.enter_context(tc.tile_pool(name="wgp", bufs=2))
        slabs = ctx.enter_context(tc.tile_pool(name="slabs", bufs=7))
        tps = ctx.enter_context(tc.psum_pool(name="tps", bufs=3))
        accp = ctx.enter_context(tc.psum_pool(name="accp", bufs=5))
        ctx.enter_context(tc.manual_schedule(engines={mybir.EngineType.PE, mybir.EngineType.DVE,
                                                      mybir.EngineType.Activation, mybir.EngineType.Pool}))

        xs_col = const.tile([P, PASSES, 4], F32, name="xs_col")
        nc.sync.dma_start(out=xs_col[:], in_=x_scale.rearrange("a b k -> (a b k)").rearrange("(g p t) -> p g t", p=P, t=4))
        xb_view = x_bytes.rearrange("b (a p) k -> a p b k", p=P)
        xbytes = []
        for a in range(POS_TILES):
            xbytes_a = const.tile([P, B, D], U8, name="xbytes%d" % a)
            xbytes.append(xbytes_a)
        wraw = []

        def load_x(a):
            nc.sync.dma_start(out=xbytes[a][:], in_=xb_view[a])

        def load_w(c):
            src = weights[c // 2].rearrange("(h v p z) k -> h p v z k", h=2, v=2, z=2)
            wraw_c = slabs.tile([P, 2, 2, D], BF16, name="slab")
            wraw.append(wraw_c)
            nc.sync.dma_start(out=wraw_c[:], in_=src[c % 2])

        load_w(0)
        load_x(0)
        load_x(1)
        load_w(1)
        load_w(2)
        load_w(3)
        load_x(2)
        load_x(3)

        zeros = const.tile([P, 512], BF16, name="zeros")
        nc.gpsimd.memset(zeros[:], 0.0)

        def keep_clock():
            acc = accp.tile([P, 512], F32, name="acc")
            nc.tensor.matmul(acc[:], lhsT=zeros[:, 0:P], rhs=zeros[:], start=True, stop=True)

        tcol = const.tile([P, POS_TILES], F32, name="tcol")
        nc.gpsimd.iota(tcol[:], pattern=[[P, POS_TILES]], base=0, channel_multiplier=1,
                       allow_small_or_imprecise_dtypes=True)
        ident = const.tile([P, P], F32, name="ident")
        make_identity(nc, ident[:])
        inv = const.tile([P, PAIRS], F32, name="inv")
        nc.vector.memset(inv[:, 0:1], 1.0)
        first_sin = const.tile([P, 1], F32, name="first_sin")
        nc.scalar.activation(out=first_sin[:], in_=inv[:, 0:1], func=ACT.Sin)
        turns = const.tile([P, POS_TILES], F32, name="turns")
        back = const.tile([P, POS_TILES], F32, name="back")
        n = 1
        while n < PAIRS:
            for q in range(1, min(4, PAIRS // n)):
                nc.vector.tensor_scalar(out=inv[:, q * n:(q + 1) * n], in0=inv[:, 0:n],
                                        scalar1=THETA ** (-q * n / float(PAIRS)), scalar2=None, op0=ALU.mult)
            n *= 4
            if n == 4:
                nc.vector.tensor_scalar(out=turns[:], in0=tcol[:], scalar1=1.0 / TWO_PI, scalar2=None, op0=ALU.mult)
            if n == 16:
                nc.vector.tensor_scalar(out=back[:], in0=tcol[:], scalar1=-1.0 / TWO_PI, scalar2=None, op0=ALU.mult)

        args = {}
        tabs = {}
        whole = {}

        def whole_turns(a):
            whole_a = const.tile([P, REDUCED], I32, name="ni%d" % a)
            whole[a] = whole_a
            nc.vector.tensor_scalar(out=whole[a][:], in0=inv[:, 0:REDUCED], scalar1=turns[:, a:a + 1], scalar2=None,
                                    op0=ALU.mult)

        def turns_left(a, first, last, plane, col, op):
            if plane == 2:
                arg_new = argp.tile([P, 3, last - first], F32, name="arg%d" % (last - first))
                args[a, first // HALF] = arg_new
            arg = args[a, first // HALF]
            if first < REDUCED:
                stop = min(last, REDUCED)
                nc.vector.scalar_tensor_tensor(out=arg[:, plane, 0:stop - first], in0=inv[:, first:stop],
                                               scalar=col[:, a:a + 1], in1=whole[a][:, first:stop], op0=ALU.mult,
                                               op1=op)
            if last > REDUCED:
                nc.vector.tensor_scalar(out=arg[:, plane, REDUCED - first:last - first], in0=inv[:, REDUCED:last],
                                        scalar1=col[:, a:a + 1], scalar2=None, op0=ALU.mult)

        def table_turns(a):
            whole_turns(a)
            turns_left(a, 0, PAIRS, 2, turns, ALU.subtract)

        def half_table_turns(a, h):
            turns_left(a, h * HALF, (h + 1) * HALF, 2, turns, ALU.subtract)
            turns_left(a, h * HALF, (h + 1) * HALF, 0, back, ALU.add)

        def quarter_min(a, h):
            arg = args[a, h]
            nc.vector.tensor_tensor(out=arg[:, 1, :], in0=arg[:, 2, :], in1=arg[:, 0, :], op=ALU.min)

        def quarter_add(a, h):
            arg = args[a, h]
            nc.vector.tensor_scalar(out=arg[:, 1, :], in0=arg[:, 1, :], scalar1=0.25, scalar2=None, op0=ALU.add)

        def planes_on_scalar(a, h=0):
            arg = args[a, h]
            nc.scalar.activation(out=arg[:, 0, :], in_=arg[:, 2, :], func=ACT.Copy, scale=-1.0)
            nc.scalar.activation(out=arg[:, 1, :], in_=arg[:, 2, :], func=ACT.Abs)
            nc.scalar.activation(out=arg[:, 1, :], in_=arg[:, 1, :], func=ACT.Identity, scale=-1.0, bias=0.25)

        def tables(a, halves):
            if halves.start == 0:
                tab = tabp.tile([P, 2, 2, HALF, 2], F32, name="tab")
                tabs[a] = tab
            for z in range(2):
                planes_read = args[a, halves.start][:, 1 - z:3 - z, :]
                nc.scalar.activation(out=tabs[a][:, halves, z, :, :],
                                     in_=planes_read.rearrange("p e (h i) -> p h i e", i=HALF), func=ACT.Sin,
                                     scale=TWO_PI)

        xs_bc = const.tile([P, D], F32, name="xs_bc")

        def spread_scales(g):
            tp = tps.tile([P, 4, P], F32, name="tp")
            for t in range(4):
                nc.tensor.transpose(tp[:, t, :], xs_col[:, g, t:t + 1].to_broadcast([P, P]), ident[:])
            nc.scalar.copy(out=xs_bc[:, 512 * g:512 * (g + 1)].rearrange("p (n t) -> p n t", t=4),
                                  in_=tp[:].rearrange("p t n -> p n t"))

        def transpose_words(src):
            tp = tps.tile([P, 2 * PASSES, P], F32, name="tp")
            words = src.bitcast(F32)
            for g in range(PASSES):
                for u in range(2):
                    nc.tensor.transpose(tp[:, 2 * g + u, :], words[:, 256 * g + u:256 * (g + 1):2], ident[:])
            return tp

        xcodes, xscales = [], []
        for a in range(POS_TILES):
            xc_a = const.tile([P, B * PASSES * P], U32, name="xc%d" % a, align_bytes=64)
            xs_a = const.tile([P, B * PASSES * P], U8, name="xs%d" % a, align_bytes=64)
            xcodes.append(xc_a)
            xscales.append(xs_a)

        widened, grouped = {}, {}

        def widen(b):
            xw = xwp.tile([P, D], BF16, name="xw")
            nc.vector.tensor_tensor(out=xw[:], in0=xbytes[0][:, b, :].bitcast(FP8), in1=xs_bc[:], op=ALU.mult)
            widened[b] = xw

        def turn_x(b):
            tp = transpose_words(widened[b][:])
            xg = xgp.tile([P, PASSES * P * 4], BF16, name="xg", align_bytes=64)
            nc.scalar.copy(out=xg[:].bitcast(F32).rearrange("p (g r u) -> p g r u", g=PASSES, u=2),
                           in_=tp[:].rearrange("p (g u) r -> p g r u", g=PASSES))
            grouped[b] = xg

        def quant_x(b):
            cols = slice(b * PASSES * P, (b + 1) * PASSES * P)
            nc.vector.quantize_mx(out=xcodes[0][:, cols].bitcast(FP8X4), scales=xscales[0][:, cols], in_=grouped[b][:])

        casts, grouped4 = {}, {}

        def cast_group(a, engine_copy):
            xcast = xcp.tile([P, B, D], BF16, name="xcast")
            for b in range(B):
                engine_copy(out=xcast[:, b, :], in_=xbytes[a][:, b, :].bitcast(FP8))
            casts[a] = xcast

        planes = {}

        def bank(a, k):
            g, u = k // 2, k % 2
            if k == 0:
                planes_new = xplp.tile([P, PASSES, 4, B * P], BF16, name="xpl")
                planes[a] = planes_new
            tp = tps.tile([P, B, P], F32, name="tp")
            for b in range(B):
                words = casts[a][:, b, :].bitcast(F32)
                nc.tensor.transpose(tp[:, b, :], words[:, 256 * g + u:256 * (g + 1):2], ident[:])
            halves = tp[:].rearrange("p b r -> p (b r)").bitcast(BF16).rearrange("p (b r e) -> p b r e", b=B, e=2)
            for e in range(2):
                t = 2 * u + e
                nc.scalar.activation(out=planes[a][:, g, t, :].rearrange("p (b r) -> p b r", b=B),
                                     in_=halves[:, :, :, e], func=ACT.Copy, scale=xs_col[:, g, t:t + 1])
            if u == 1:
                if g == 0:
                    xg4_new = xg4p.tile([P, B * PASSES * P * 4], BF16, name="xg4", align_bytes=64)
                    grouped4[a] = xg4_new
                width = B * P * 4
                nc.scalar.copy(out=grouped4[a][:, g * width:(g + 1) * width].rearrange("p (c i t) -> p c t i", i=4, t=4),
                               in_=planes[a][:, g, :, :].rearrange("p t (c i) -> p c t i", i=4))

        def quant_group(a, g):
            cols = slice(g * B * P, (g + 1) * B * P)
            nc.vector.quantize_mx(out=xcodes[a][:, cols].bitcast(FP8X4), scales=xscales[a][:, cols],
                                  in_=grouped4[a][:, 4 * cols.start:4 * cols.stop])

        wcodes, wscales, wgrouped = {}, {}, {}

        def turn_w(c, r, engine_copy):
            if r == 0:
                wg_new = wgp.tile([P, PASSES * 512 * 4], BF16, name="wg", align_bytes=64)
                wgrouped[c] = wg_new
            g, z = r // 2, r % 2
            tp = tps.tile([P, 4, P], F32, name="tp")
            for v in range(2):
                words = wraw[c][:, v, z, :].bitcast(F32)
                for u in range(2):
                    nc.tensor.transpose(tp[:, 2 * v + u, :], words[:, 256 * g + u:256 * (g + 1):2], ident[:])
            stretch = slice((2 * g + z) * 512, (2 * g + z + 1) * 512)
            engine_copy(out=wgrouped[c][:].bitcast(F32)[:, stretch].rearrange("p (v r u) -> p v r u", v=2, u=2),
                        in_=tp[:].rearrange("p (v u) r -> p v r u", v=2))

        def quant_w(c, passes):
            if passes.start == 0:
                wc = const.tile([P, PASSES * 512], U32, name="wc%d" % c, align_bytes=64)
                ws = const.tile([P, PASSES * 512], U8, name="ws%d" % c, align_bytes=64)
                wcodes[c] = wc
                wscales[c] = ws
            cols = slice(passes.start * 512, passes.stop * 512)
            nc.vector.quantize_mx(out=wcodes[c][:, cols].bitcast(FP8X4), scales=wscales[c][:, cols],
                                  in_=wgrouped[c][:, 4 * cols.start:4 * cols.stop])

        pieces = [(0, b, c) for c in range(4) for b in range(B)]
        pieces += [(a, b, c) for a in range(1, POS_TILES) for b in range(B) for c in range(4)]
        banks = {}

        def mm(j):
            a, b, c = pieces[j]
            acc = accp.tile([P, 512], F32, name="acc")
            for g in range(PASSES):
                first = (b * PASSES + g) * P if a == 0 else (g * B + b) * P
                cols = slice(first, first + P)
                nc.tensor.matmul_mx(
                    out=acc[:],
                    lhsT=xcodes[a][:, cols].bitcast(FP8X4),
                    lhsT_scale=xscales[a][:, cols],
                    rhs=wcodes[c][:, g * 512:(g + 1) * 512].bitcast(FP8X4),
                    rhs_scale=wscales[c][:, g * 512:(g + 1) * 512],
                    start=(g == 0),
                    stop=(g == PASSES - 1),
                )
            banks[j] = acc

        products = {}
        waiting = []
        behind_one = []

        def by_vector(j):
            return j == len(pieces) - 2

        def by_tensor(j):
            return j % TENSOR_EVERY == 2 and TENSOR_FROM <= j < len(pieces) - 2

        def store(a, b, m, first, tile_ap):
            nc.sync.dma_start(out=outs[m][b, a * P:(a + 1) * P, first:first + tile_ap.shape[1]], in_=tile_ap)

        def add_on_tensor(a, b, m, h, prod):
            tp = tps.tile([P, 4, P], F32, name="tp")
            total = tp[:].rearrange("p v r -> p (v r)")
            for z in range(2):
                nc.tensor.matmul(total, lhsT=ident[:], rhs=prod[:, z, :], start=(z == 0), stop=(z == 1))
            nc.scalar.copy(out=prod[:, 0, :], in_=total)
            store(a, b, m, h * 512, prod[:, 0, :])

        def tensor_sums(j):
            while waiting and waiting[0][0] <= j - 2:
                add_on_tensor(*waiting.pop(0)[1])

        def multiply(a, h, first, last, out, bank_cols):
            nc.vector.tensor_tensor(
                out=out.rearrange("p z (i e) -> p z i e", e=2),
                in0=tabs[a][:, h, :, first:last, :],
                in1=bank_cols[:, :, first:last].unsqueeze(3).to_broadcast([P, 2, last - first, 2]),
                op=ALU.mult)

        def add(prod, engine_add):
            engine_add(out=prod[:, 0, :], in0=prod[:, 0, :], in1=prod[:, 1, :], op=ALU.add)

        def vector_sums():
            for a, b, m, h, prod in behind_one:
                add(prod, nc.vector.tensor_tensor)
                store(a, b, m, h * 512, prod[:, 0, :])
            behind_one.clear()

        def vg(j):
            a, b, c = pieces[j]
            m, h = c // 2, c % 2
            bank_cols = banks[j][:].rearrange("p (z i) -> p z i", z=2)
            if j == len(pieces) - 1:
                ends = []
                for s in range(2):
                    end = slabs.tile([P, 2, HALF], F32, name="slab")
                    multiply(a, h, s * P, (s + 1) * P, end[:], bank_cols)
                    ends.append(end)
                vector_sums()
                for s in range(2):
                    add(ends[s][:], nc.vector.tensor_tensor)
                    store(a, b, m, h * 512 + s * HALF, ends[s][:, 0, :])
                return
            if h == 0:
                prod_new = slabs.tile([P, 2, 2, 512], F32, name="slab")
                products[(a, b, m)] = prod_new
            prod = products[(a, b, m)][:, h, :, :]
            multiply(a, h, 0, HALF, prod, bank_cols)
            vector_sums()
            if by_tensor(j):
                waiting.append((j, (a, b, m, h, prod)))
            elif by_vector(j):
                behind_one.append((a, b, m, h, prod))
            else:
                add(prod, nc.gpsimd.tensor_tensor)
                store(a, b, m, h * 512, prod[:, 0, :])


        s_copy, v_copy = nc.scalar.copy, nc.vector.tensor_copy

        def make_table(a):
            planes_on_scalar(a)
            tables(a, slice(0, 2))

        cast_group(1, nc.gpsimd.tensor_copy)
        whole_turns(0)
        half_table_turns(0, 0)
        whole_turns(1)
        quarter_min(0, 0)
        whole_turns(2)
        quarter_add(0, 0)
        whole_turns(3)
        turns_left(1, 0, PAIRS, 2, turns, ALU.subtract)
        keep_clock()
        keep_clock()
        keep_clock()
        keep_clock()
        spread_scales(0)
        spread_scales(1)
        keep_clock()
        keep_clock()
        turn_w(0, 0, s_copy)
        turn_w(0, 1, s_copy)
        keep_clock()
        turn_w(0, 2, s_copy)
        turn_w(0, 3, s_copy)
        keep_clock()
        tables(0, slice(0, 1))
        widen(0)
        turn_x(0)
        keep_clock()
        keep_clock()
        half_table_turns(0, 1)
        quant_w(0, slice(0, 1))
        quarter_min(0, 1)
        quant_w(0, slice(1, 2))
        quarter_add(0, 1)
        turn_w(1, 0, s_copy)
        turn_w(1, 1, s_copy)
        keep_clock()
        turn_w(1, 2, s_copy)
        turn_w(1, 3, s_copy)
        keep_clock()
        widen(1)
        quant_x(0)
        mm(0)
        turn_x(1)
        widen(2)
        turn_x(2)
        turn_w(2, 0, s_copy)
        turn_w(2, 1, s_copy)
        vg(0)
        quant_x(1)
        mm(1)
        widen(3)
        turn_w(2, 2, s_copy)
        turn_w(2, 3, s_copy)
        turn_x(3)
        vg(1)
        quant_x(2)
        mm(2)
        quant_w(1, slice(0, 2))
        tables(0, slice(1, 2))
        turn_w(3, 0, s_copy)
        turn_w(3, 1, s_copy)
        quant_x(3)
        mm(3)
        vg(2)
        turn_w(3, 2, s_copy)
        turn_w(3, 3, s_copy)
        mm(4)
        vg(3)
        bank(1, 0)
        mm(5)
        vg(4)
        mm(6)
        bank(1, 1)
        turns_left(2, 0, PAIRS, 2, turns, ALU.subtract)
        quant_w(2, slice(0, 2))
        vg(5)
        mm(7)
        bank(1, 2)
        make_table(1)

        before = {8: [(quant_w, (3, slice(0, 2)))], 13: [(turns_left, (3, 0, PAIRS, 2, turns, ALU.subtract))]}
        behind = {6: [(bank, (1, 3))]}
        for a in range(1, POS_TILES):
            before[16 * a - LATE] = [(quant_group, (a, 0)), (quant_group, (a, 1))]
        for a in range(2, POS_TILES):
            first = 16 * (a - 1)
            behind[first - 4] = [(cast_group, (a, s_copy))]
            for k, step in enumerate((0, 1, 3, 5)):
                behind[first + step] = [(bank, (a, k))]
            behind[first + 6] = [(make_table, (a,))]
        mm_next = 8
        for j in range(6, len(pieces)):
            for step, what in before.get(j, []):
                step(*what)
            vg(j)
            while mm_next < len(pieces) and mm_next <= j + AHEAD and j >= 16 * pieces[mm_next][0] - LATE:
                mm(mm_next)
                mm_next += 1
            tensor_sums(j)
            for step, what in behind.get(j, []):
                step(*what)
